import numpy as np
import ml_dtypes


def mxq(x, axis, fmt="e4m3"):
    dtype, down = {"e4m3": (ml_dtypes.float8_e4m3fn, 7), "e5m2": (ml_dtypes.float8_e5m2, 14)}[fmt]
    v = np.moveaxis(np.asarray(x, np.float32).astype(ml_dtypes.bfloat16).astype(np.float64), axis, -1)
    blocks = v.reshape(v.shape[:-1] + (-1, 32))
    amax = np.abs(blocks).max(-1, keepdims=True)
    byte = np.maximum(np.where(amax > 0, np.frexp(amax)[1] - 1 + 127, 0) - down, 1)
    scale = np.exp2(byte - 127.0)
    codes = (blocks / scale).astype(np.float32).astype(dtype).astype(np.float64)
    return np.moveaxis((codes * scale).reshape(v.shape), -1, axis)


WIDE = False


def mx_kscale(k):
    if not WIDE:
        return np.ones(k)
    levels = np.array([10, -10, 5, -5, 0])
    a = np.random.permutation(np.resize(levels, k // 512 * 4)).reshape(k // 512, 4)
    idx = np.arange(k)
    return np.exp2(a[idx // 512, idx % 128 // 32])


BF16 = ml_dtypes.bfloat16


def bf(x):
    return np.asarray(x, np.float32).astype(BF16)


def f64(x):
    return np.asarray(x).astype(np.float64)


B, T, D, H, FF, V = 1, 512, 512, 4, 2048, 2048
HD = D // H
EPS = 1e-5
ERF_MAX, ERF_TERMS = 6.0, 120


def erf(x):
    z = np.clip(x, -ERF_MAX, ERF_MAX)
    zz = 2.0 * z * z
    term = z.copy()
    acc = z.copy()
    for n in range(1, ERF_TERMS):
        term = term * zz / (2.0 * n + 1.0)
        acc = acc + term
    return 2.0 / np.sqrt(np.pi) * np.exp(-z * z) * acc


def gelu_erf(v):
    return 0.5 * v * (1.0 + erf(v / np.sqrt(2.0)))


def layernorm(x, w, b):
    mu = x.mean(-1, keepdims=True)
    var = np.square(x - mu).mean(-1, keepdims=True)
    return (x - mu) / np.sqrt(var + EPS) * w + b


def setup_inputs():
    r = np.random.standard_normal
    s = mx_kscale(D)
    return {"xt_new": bf(r((B, T, D))), "xe": bf(r((B, T, D))),
            "ln2_w": bf((1.0 + 0.1 * r(D)) * s), "ln2_b": bf(0.1 * r(D) * s),
            "fc_w": bf(r((H, FF, D)) / np.sqrt(D) / s), "fc_b": bf(0.3 * r((H, FF))),
            "proj_w": bf(r((H, HD, FF)) * 1.5 / np.sqrt(FF)), "proj_b": bf(0.3 * r((H, HD))),
            "dln_w": bf(1.0 + 0.1 * r((H, HD))), "dln_b": bf(0.1 * r((H, HD)))}


def reference(xt_new, xe, ln2_w, ln2_b, fc_w, fc_b, proj_w, proj_b, dln_w, dln_b):
    x2 = layernorm(f64(xt_new) + f64(xe), f64(ln2_w), f64(ln2_b))
    x2q = mxq(x2, 2, "e4m3")
    a = (x2q[:, None] @ mxq(f64(fc_w), 2, "e4m3").transpose(0, 2, 1)) + f64(fc_b)[None, :, None, :]
    g = gelu_erf(a)
    p = (mxq(g, 3, "e4m3") @ mxq(f64(proj_w), 2, "e4m3").transpose(0, 2, 1)) + f64(proj_b)[None, :, None, :]
    return layernorm(p, f64(dln_w)[None, :, None, :], f64(dln_b)[None, :, None, :])

@@ -1,0 +1,449 @@
+from contextlib import ExitStack
+
+import concourse.mybir as mybir
+from concourse.masks import make_identity
+
+F32 = mybir.dt.float32
+BF16 = mybir.dt.bfloat16
+U32 = mybir.dt.uint32
+U8 = mybir.dt.uint8
+FP8X4 = mybir.dt.float8_e4m3fn_x4
+ACT = mybir.ActivationFunctionType
+ALU = mybir.AluOpType
+
+P = 128
+T = 512
+D = 512
+H = 4
+FF = 2048
+HD = 128
+EPS = 1e-5
+NJ = T // P
+NC = FF // 512
+FLOPS = 2 * T * D * FF * H + 2 * T * FF * HD * H
+
+PROG = "ttccafansttccansttccannssrQrQttrQqccrQqttcc!ggggqqcCcggggRqGqcCcggggRqGqcCcggggRqGcCcggggRqGqcCcggggRqGcCcPggggRqGqcc12ggggRqGcc34ggggRqGccggggRqGccPggggRqGcc12ggggRqGcc34ggggRqGggggRGPggggRG12ggggRG34ggggRGPRG12P312434"
+NTR = 3
+NFC = 4
+PJ_POS = {6: 0, 11: 1, 16: 2, 19: 3}
+TAPER = True
+BC_AFTER = 9
+
+
+def tile_tftdictblock_pa_kernel(
+    tc, xt_new, xe, ln2_w, ln2_b, fc_w, fc_b, proj_w, proj_b, dln_w, dln_b, out
+):
+    nc = tc.nc
+    with ExitStack() as ctx:
+        const = ctx.enter_context(tc.tile_pool(name="const", bufs=1))
+        xpool = ctx.enter_context(tc.tile_pool(name="xpool", bufs=1))
+        small = ctx.enter_context(tc.tile_pool(name="small", bufs=4))
+        rawp = ctx.enter_context(tc.tile_pool(name="rawp", bufs=12))
+        wgp = ctx.enter_context(tc.tile_pool(name="wgp", bufs=8))
+        wcp = ctx.enter_context(tc.tile_pool(name="wcp", bufs=12))
+        pcp = ctx.enter_context(tc.tile_pool(name="pcp", bufs=4))
+        gpp = ctx.enter_context(tc.tile_pool(name="gpp", bufs=3))
+        ggp = ctx.enter_context(tc.tile_pool(name="ggp", bufs=2))
+        gcp = ctx.enter_context(tc.tile_pool(name="gcp", bufs=8))
+        fin = ctx.enter_context(tc.tile_pool(name="fin", bufs=2))
+        ps_tr = ctx.enter_context(tc.psum_pool(name="ps_tr", bufs=NTR))
+        ps_fc = ctx.enter_context(tc.psum_pool(name="ps_fc", bufs=NFC))
+        ps_pj = ctx.enter_context(tc.psum_pool(name="ps_pj", bufs=1))
+        ctx.enter_context(tc.manual_schedule())
+
+        units = []
+        quad = 0
+        for pos in range(20):
+            if pos in PJ_POS:
+                units.append(("pj", PJ_POS[pos]))
+            else:
+                units.append(("fc", quad))
+                quad += 1
+        unit_of_quad = {}
+        unit_of_head = {}
+        for pos, (kind, idx) in enumerate(units):
+            if kind == "fc":
+                unit_of_quad[idx] = pos
+            else:
+                unit_of_head[idx] = pos
+
+        vec_a = const.tile([P, 512], BF16, name="vec_a")
+        nc.vector.memset(vec_a[:], 0.0)
+        nc.scalar.dma_start(out=vec_a[0:1, :], in_=ln2_w.rearrange("(o d) -> o d", o=1))
+        nc.scalar.dma_start(out=vec_a[1:2, :], in_=ln2_b.rearrange("(o d) -> o d", o=1))
+        nc.scalar.dma_start(out=vec_a[8:24, :], in_=fc_b.rearrange("h (c x) -> (h c) x", x=512))
+        warm_in = const.tile([P, 1], F32, name="warm_in")
+        warm_out = const.tile([P, 1], F32, name="warm_out")
+        nc.vector.memset(warm_in[:], 0.0)
+        nc.scalar.activation(out=warm_out[:], in_=warm_in[:], func=ACT.Gelu)
+        neg_half1 = const.tile([P, 1], F32, name="neg_half1")
+        neg_half4 = const.tile([P, NJ, 1], F32, name="neg_half4")
+        nc.vector.memset(neg_half1[:], -0.5)
+        nc.vector.memset(neg_half4[:], -0.5)
+        ident_bf = const.tile([P, P], BF16, name="ident_bf")
+        ident_f = const.tile([P, P], F32, name="ident_f")
+        make_identity(nc, ident_bf[:])
+        make_identity(nc, ident_f[:])
+
+        xt_v = xt_new.rearrange("b (p j) d -> p (b j) d", j=NJ)
+        xe_v = xe.rearrange("b (p j) d -> p (b j) d", j=NJ)
+        xt_sb = xpool.tile([P, NJ, D], BF16, name="xt_sb")
+        xe_sb = xpool.tile([P, NJ, D], BF16, name="xe_sb")
+        raws = []
+        tail_bc = []
+
+        def load_x(half):
+            js = slice(2 * half, 2 * half + 2)
+            nc.sync.dma_start(out=xt_sb[:, js, :], in_=xt_v[:, js, :])
+            nc.sync.dma_start(out=xe_sb[:, js, :], in_=xe_v[:, js, :])
+
+        def load_unit(pos):
+            kind, idx = units[pos]
+            raw = rawp.tile([P, 2048], BF16, name="raw", tag="raw")
+            if kind == "fc":
+                h, c = divmod(idx, NC)
+                nc.sync.dma_start(
+                    out=raw[:].rearrange("p (u x) -> p u x", u=2),
+                    in_=fc_w[h, 512 * c : 512 * (c + 1), :].rearrange("(u p e) k -> p u (e k)", u=2, e=2),
+                )
+            else:
+                nc.sync.dma_start(out=raw[:], in_=proj_w[idx, :, :])
+            raws.append(raw)
+
+        load_x(0)
+        load_unit(0)
+        load_x(1)
+        for pos in range(1, 20):
+            load_unit(pos)
+            if pos == BC_AFTER:
+                for r, vec in enumerate((proj_b, dln_w, dln_b)):
+                    bc = const.tile([P, 512], BF16, name="bc%d" % r)
+                    nc.sync.dma_start(out=bc[:], in_=vec.rearrange("h d -> (h d)").partition_broadcast(P))
+                    tail_bc.append(bc)
+        pb_bc, dw_bc, db_bc = tail_bc
+
+        vec_a2 = const.tile([P, 512], BF16, name="vec_a2")
+        nc.vector.tensor_copy(
+            out=vec_a2[:].rearrange("p (u e q) -> p u e q", u=2, e=2),
+            in_=vec_a[:].rearrange("p (u q e) -> p u e q", u=2, e=2),
+        )
+        cols_ps = ps_pj.tile([P, 4, P], BF16, name="cols_ps", tag="pj")
+        for t in range(4):
+            nc.tensor.transpose(cols_ps[:, t, :], vec_a2[:, P * t : P * (t + 1)], ident_bf[:])
+        cols = const.tile([P, 4, 24], F32, name="cols")
+
+        x2p = xpool.tile([P, 4, T], BF16, name="x2p")
+        x2g = xpool.tile([P, T, 4], BF16, name="x2g", align_bytes=64)
+        xc = xpool.tile([P, T], U32, name="xc", align_bytes=64)
+        xs = xpool.tile([P, T], U8, name="xs", align_bytes=64)
+
+        gelus = []
+        rg_pieces = []
+        for r in range(16):
+            if TAPER and r == 15:
+                for half in range(2):
+                    for t in range(4):
+                        gelus.append((r, t, 2 * half, 2 * half + 2))
+                rg_pieces.append((r, 0, 2))
+                rg_pieces.append((r, 2, 4))
+            else:
+                for t in range(4):
+                    gelus.append((r, t, 0, 4))
+                rg_pieces.append((r, 0, 4))
+        head_pieces = []
+        for h in range(H):
+            if TAPER and h == H - 1:
+                head_pieces.append((h, 0, 2))
+                head_pieces.append((h, 2, 4))
+            else:
+                head_pieces.append((h, 0, 4))
+
+        k = {}
+        for key in "TCqFgRGPanxrQ1234!":
+            k[key] = 0
+        tr_t = {}
+        wg_t = {}
+        w_ops = {}
+        a_t = {}
+        gp_t = {}
+        gg_t = {}
+        g_ops = {}
+        x_t = {}
+        ln_t = {}
+
+        def emit_t():
+            u, b = divmod(k["T"], 2)
+            raw32 = raws[u][:].bitcast(F32)
+            tr = ps_tr.tile([P, 512], F32, name="tr", tag="tr")
+            for q in range(4):
+                blk = 4 * b + q
+                nc.tensor.transpose(tr[:, P * q : P * (q + 1)], raw32[:, P * blk : P * (blk + 1)], ident_f[:])
+            tr_t[(u, b)] = tr
+            k["T"] += 1
+
+        def ahead():
+            while k["!"] > 0 and k["T"] < min(k["C"] + NTR, 40):
+                emit_t()
+
+        def emit_c(on_vector):
+            u, b = divmod(k["C"], 2)
+            while k["T"] <= k["C"]:
+                emit_t()
+            if b == 0:
+                wg = wgp.tile([P, 2048], BF16, name="wg", tag="wg", align_bytes=64)
+                wg_t[u] = wg
+            dst = wg_t[u][:].bitcast(F32)[:, 512 * b : 512 * (b + 1)].rearrange("p (i f u) -> p i f u", i=2, u=2)
+            src = tr_t[(u, b)][:].rearrange("p (i u f) -> p i f u", i=2, u=2)
+            if on_vector:
+                nc.vector.tensor_copy(out=dst, in_=src)
+            else:
+                nc.scalar.copy(out=dst, in_=src)
+            k["C"] += 1
+            ahead()
+
+        def emit_qw():
+            u = k["q"]
+            pool = wcp if units[u][0] == "fc" else pcp
+            codes = pool.tile([P, 512], U32, name="codes", tag="codes", align_bytes=64)
+            scales = pool.tile([P, 512], U8, name="scales", tag="scales", align_bytes=64)
+            nc.vector.quantize_mx(out=codes[:].bitcast(FP8X4), scales=scales[:], in_=wg_t[u][:])
+            w_ops[u] = (codes, scales)
+            k["q"] += 1
+
+        def can_f():
+            if k["F"] >= 64 or k["Q"] < NJ:
+                return False
+            if unit_of_quad[k["F"] // 4] >= k["q"]:
+                return False
+            return k["F"] < done_gelus() + NFC
+
+        def done_gelus():
+            n = 0
+            for r, t, j0, j1 in gelus[: k["g"]]:
+                if j1 == NJ:
+                    n += 1
+            return n
+
+        def emit_f():
+            r, t = divmod(k["F"], 4)
+            wc, ws = w_ops[unit_of_quad[r]]
+            a_ps = ps_fc.tile([P, T], F32, name="a_ps", tag="fc")
+            cs = slice(P * t, P * (t + 1))
+            nc.tensor.matmul_mx(
+                out=a_ps[:], lhsT=wc[:, cs].bitcast(FP8X4), lhsT_scale=ws[:, cs],
+                rhs=xc[:].bitcast(FP8X4), rhs_scale=xs[:], start=True, stop=True,
+            )
+            a_t[(r, t)] = a_ps
+            k["F"] += 1
+
+        def emit_g():
+            r, t, j0, j1 = gelus[k["g"]]
+            while (r, t) not in a_t:
+                emit_f()
+            if r not in gp_t:
+                gp = gpp.tile([P, 4, T], BF16, name="gp", tag="gp")
+                gp_t[r] = gp
+            ns = slice(P * j0, P * j1)
+            nc.scalar.activation(
+                out=gp_t[r][:, t, ns], in_=a_t[(r, t)][:, ns], func=ACT.Gelu,
+                bias=cols[:, t, 8 + r : 9 + r], scale=1.0,
+            )
+            k["g"] += 1
+            while can_f():
+                emit_f()
+
+        def emit_rg():
+            r, j0, j1 = rg_pieces[k["R"]]
+            if r not in gg_t:
+                gg = ggp.tile([P, T, 4], BF16, name="gg", tag="gg", align_bytes=64)
+                gg_t[r] = gg
+            ns = slice(P * j0, P * j1)
+            nc.vector.tensor_copy(
+                out=gg_t[r][:, ns, :].rearrange("p (n i) t -> p n t i", i=4),
+                in_=gp_t[r][:, :, ns].rearrange("p t (n i) -> p n t i", i=4),
+            )
+            k["R"] += 1
+
+        def emit_qg():
+            r, j0, j1 = rg_pieces[k["G"]]
+            if r not in g_ops:
+                gc = gcp.tile([P, T], U32, name="gc", tag="gc", align_bytes=64)
+                gs = gcp.tile([P, T], U8, name="gs", tag="gs", align_bytes=64)
+                g_ops[r] = (gc, gs)
+            gc, gs = g_ops[r]
+            ns = slice(P * j0, P * j1)
+            nc.vector.quantize_mx(
+                out=gc[:, ns].bitcast(FP8X4), scales=gs[:, ns],
+                in_=gg_t[r][:, ns, :].rearrange("p n t -> p (n t)"),
+            )
+            k["G"] += 1
+
+        def emit_p():
+            h, j0, j1 = head_pieces[k["P"]]
+            pc, pscale = w_ops[unit_of_head[h]]
+            if j0 == 0:
+                p_ps = ps_pj.tile([P, j1 - j0, HD], F32, name="p_ps", tag="pj")
+            else:
+                p_ps = ps_tr.tile([P, j1 - j0, HD], F32, name="p_ps2", tag="tr")
+            for j in range(j0, j1):
+                for c in range(NC):
+                    gc, gs = g_ops[NC * h + c]
+                    nc.tensor.matmul_mx(
+                        out=p_ps[:, j - j0, :],
+                        lhsT=gc[:, P * j : P * (j + 1)].bitcast(FP8X4), lhsT_scale=gs[:, P * j : P * (j + 1)],
+                        rhs=pc[:, P * c : P * (c + 1)].bitcast(FP8X4), rhs_scale=pscale[:, P * c : P * (c + 1)],
+                        start=(c == 0), stop=(c == NC - 1),
+                    )
+            ln_t[("p", k["P"])] = p_ps
+            k["P"] += 1
+
+        def emit_ln(stage):
+            i = k[stage]
+            h, j0, j1 = head_pieces[i]
+            n = j1 - j0
+            hd = slice(HD * h, HD * (h + 1))
+            if stage == "1":
+                pb = fin.tile([P, n, HD], F32, name="pb", tag="pb")
+                nc.vector.tensor_tensor(
+                    out=pb[:], in0=ln_t[("p", i)][:], in1=pb_bc[:, hd].unsqueeze(1).to_broadcast([P, n, HD]), op=ALU.add
+                )
+                ln_t[("pb", i)] = pb
+            elif stage == "2":
+                pb = ln_t[("pb", i)]
+                st4 = small.tile([P, n, 6], F32, name="st4", tag="st4")
+                mv4 = small.tile([P, n, 2], F32, name="mv4", tag="mv4")
+                for j in range(n):
+                    nc.vector.bn_stats(out=st4[:, j, :], in_=pb[:, j, :])
+                for j in range(n):
+                    nc.vector.bn_aggr(out=mv4[:, j, :], in_=st4[:, j, :])
+                ve4 = small.tile([P, n, 1], F32, name="ve4", tag="ve4")
+                nc.vector.tensor_scalar(out=ve4[:], in0=mv4[:, :, 1:2], scalar1=EPS, scalar2=None, op0=ALU.add)
+                rs4 = small.tile([P, n, 1], F32, name="rs4", tag="rs4")
+                nc.gpsimd.tensor_tensor(out=rs4[:], in0=ve4[:], in1=neg_half4[:, 0:n, :], op=ALU.pow)
+                ln_t[("mv", i)] = mv4
+                ln_t[("rs", i)] = rs4
+            elif stage == "3":
+                pb = ln_t[("pb", i)]
+                mv4 = ln_t[("mv", i)]
+                t1 = fin.tile([P, n, HD], F32, name="t1", tag="t1")
+                for j in range(n):
+                    nc.vector.scalar_tensor_tensor(
+                        out=t1[:, j, :], in0=pb[:, j, :], scalar=mv4[:, j, 0:1], in1=dw_bc[:, hd],
+                        op0=ALU.subtract, op1=ALU.mult,
+                    )
+                ln_t[("t1", i)] = t1
+            else:
+                t1 = ln_t[("t1", i)]
+                rs4 = ln_t[("rs", i)]
+                o = fin.tile([P, n, HD], F32, name="o", tag="o")
+                for j in range(n):
+                    nc.vector.scalar_tensor_tensor(
+                        out=o[:, j, :], in0=t1[:, j, :], scalar=rs4[:, j, :], in1=db_bc[:, hd],
+                        op0=ALU.mult, op1=ALU.add,
+                    )
+                nc.sync.dma_start(out=out[0, h].rearrange("(p j) d -> p j d", j=NJ)[:, j0:j1, :], in_=o[:])
+            k[stage] += 1
+
+        def emit_xa():
+            j = k["a"]
+            s = xpool.tile([P, D], F32, name="s", tag="s", bufs=4)
+            nc.vector.tensor_tensor(
+                out=s[:].rearrange("p (u e q) -> p u e q", u=2, e=2),
+                in0=xt_sb[:, j, :].rearrange("p (u q e) -> p u e q", u=2, e=2),
+                in1=xe_sb[:, j, :].rearrange("p (u q e) -> p u e q", u=2, e=2),
+                op=ALU.add,
+            )
+            st = small.tile([P, 6], F32, name="st", tag="st")
+            nc.vector.bn_stats(out=st[:], in_=s[:])
+            mv = small.tile([P, 2], F32, name="mv", tag="mv")
+            nc.vector.bn_aggr(out=mv[:], in_=st[:])
+            ve = small.tile([P, 1], F32, name="ve", tag="ve")
+            nc.vector.tensor_scalar(out=ve[:], in0=mv[:, 1:2], scalar1=EPS, scalar2=None, op0=ALU.add)
+            rstd = small.tile([P, 1], F32, name="rstd", tag="rstd")
+            nc.gpsimd.tensor_tensor(out=rstd[:], in0=ve[:], in1=neg_half1[:], op=ALU.pow)
+            x_t[("s", j)] = (s, mv, rstd)
+            k["a"] += 1
+
+        def emit_xn():
+            j = k["n"]
+            s, mv, rstd = x_t[("s", j)]
+            xh = xpool.tile([P, D], F32, name="xh", tag="xh", bufs=2)
+            nc.vector.tensor_scalar(
+                out=xh[:], in0=s[:], scalar1=mv[:, 0:1], scalar2=rstd[:], op0=ALU.subtract, op1=ALU.mult
+            )
+            xps = ps_fc.tile([P, 4, P], F32, name="xps", tag="fc")
+            for t in range(4):
+                nc.tensor.transpose(xps[:, t, :], xh[:, P * t : P * (t + 1)], ident_f[:])
+            x_t[("ps", j)] = xps
+            k["n"] += 1
+
+        def emit_xc(on_vector):
+            j = k["x"]
+            xps = x_t[("ps", j)]
+            for t in range(4):
+                dst = x2p[:, t, P * j : P * (j + 1)]
+                if on_vector:
+                    nc.vector.tensor_scalar(
+                        out=dst, in0=xps[:, t, :], scalar1=cols[:, t, 0:1], scalar2=cols[:, t, 1:2],
+                        op0=ALU.mult, op1=ALU.add,
+                    )
+                else:
+                    nc.scalar.activation(
+                        out=dst, in_=xps[:, t, :], func=ACT.Identity, bias=cols[:, t, 1:2], scale=cols[:, t, 0:1]
+                    )
+            k["x"] += 1
+
+        def emit_xr():
+            j = k["r"]
+            ns = slice(P * j, P * (j + 1))
+            nc.vector.tensor_copy(
+                out=x2g[:, ns, :].rearrange("p (n i) t -> p n t i", i=4),
+                in_=x2p[:, :, ns].rearrange("p t (n i) -> p n t i", i=4),
+            )
+            k["r"] += 1
+
+        def emit_qx():
+            j = k["Q"]
+            ns = slice(P * j, P * (j + 1))
+            nc.vector.quantize_mx(
+                out=xc[:, ns].bitcast(FP8X4), scales=xs[:, ns], in_=x2g[:, ns, :].rearrange("p n t -> p (n t)")
+            )
+            k["Q"] += 1
+
+        for tk in PROG:
+            if tk == "t":
+                emit_t()
+            elif tk == "!":
+                k["!"] = 1
+                ahead()
+            elif tk == "c":
+                emit_c(False)
+            elif tk == "C":
+                emit_c(True)
+            elif tk == "q":
+                emit_qw()
+            elif tk == "g":
+                emit_g()
+            elif tk == "R":
+                emit_rg()
+            elif tk == "G":
+                emit_qg()
+            elif tk == "P":
+                emit_p()
+            elif tk in "1234":
+                emit_ln(tk)
+            elif tk == "a":
+                emit_xa()
+            elif tk == "n":
+                emit_xn()
+            elif tk == "s":
+                emit_xc(False)
+            elif tk == "v":
+                emit_xc(True)
+            elif tk == "r":
+                emit_xr()
+            elif tk == "Q":
+                emit_qx()
+            elif tk == "f":
+                nc.vector.tensor_copy(out=cols[:], in_=cols_ps[:, :, 0:24])
+        assert k["g"] == len(gelus) and k["4"] == len(head_pieces) and k["C"] == 40 and k["q"] == 20

@@ -22,12 +22,12 @@ NJ = T // P
 NC = FF // 512
 FLOPS = 2 * T * D * FF * H + 2 * T * FF * HD * H
 
-PROG = "ttccafansttccansttccannssrQrQttrQqccrQqttcc!ggggqqcCcggggRqGqcCcggggRqGqcCcggggRqGcCcggggRqGqcCcggggRqGcCcPggggRqGqcc12ggggRqGcc34ggggRqGccggggRqGccPggggRqGcc12ggggRqGcc34ggggRqGggggRGPggggRG12ggggRG34ggggRGPRG12P312434"
+PROG = "!eaaaannnnfsvsvrQccqccqccqccqccqggggcCcggggRqGcCcggggRqGqcCcggggRqGcCcggggRqGqcCcggggRqGcCcPggggRqGqcc12ggggRqGcc34ggggRqGccggggRqGccPggggRqGcc12ggggRqGcc34ggggRqGggggRGPggggRG12ggggRG34ggggRGPRG12P312434"
 NTR = 3
 NFC = 4
 PJ_POS = {6: 0, 11: 1, 16: 2, 19: 3}
 TAPER = True
-BC_AFTER = 9
+BC_AFTER = 13
 
 
 def tile_tftdictblock_pa_kernel(
@@ -49,7 +49,6 @@ def tile_tftdictblock_pa_kernel(
         ps_tr = ctx.enter_context(tc.psum_pool(name="ps_tr", bufs=NTR))
         ps_fc = ctx.enter_context(tc.psum_pool(name="ps_fc", bufs=NFC))
         ps_pj = ctx.enter_context(tc.psum_pool(name="ps_pj", bufs=1))
-        ctx.enter_context(tc.manual_schedule())
 
         units = []
         quad = 0
@@ -123,14 +122,16 @@ def tile_tftdictblock_pa_kernel(
         pb_bc, dw_bc, db_bc = tail_bc
 
         vec_a2 = const.tile([P, 512], BF16, name="vec_a2")
-        nc.vector.tensor_copy(
-            out=vec_a2[:].rearrange("p (u e q) -> p u e q", u=2, e=2),
-            in_=vec_a[:].rearrange("p (u q e) -> p u e q", u=2, e=2),
-        )
         cols_ps = ps_pj.tile([P, 4, P], BF16, name="cols_ps", tag="pj")
-        for t in range(4):
-            nc.tensor.transpose(cols_ps[:, t, :], vec_a2[:, P * t : P * (t + 1)], ident_bf[:])
         cols = const.tile([P, 4, 24], F32, name="cols")
+
+        def emit_e():
+            nc.vector.tensor_copy(
+                out=vec_a2[:].rearrange("p (u e q) -> p u e q", u=2, e=2),
+                in_=vec_a[:].rearrange("p (u q e) -> p u e q", u=2, e=2),
+            )
+            for t in range(4):
+                nc.tensor.transpose(cols_ps[:, t, :], vec_a2[:, P * t : P * (t + 1)], ident_bf[:])
 
         x2p = xpool.tile([P, 4, T], BF16, name="x2p")
         x2g = xpool.tile([P, T, 4], BF16, name="x2g", align_bytes=64)
@@ -211,7 +212,7 @@ def tile_tftdictblock_pa_kernel(
             k["q"] += 1
 
         def can_f():
-            if k["F"] >= 64 or k["Q"] < NJ:
+            if k["F"] >= 64 or k["Q"] < 1:
                 return False
             if unit_of_quad[k["F"] // 4] >= k["q"]:
                 return False
@@ -367,47 +368,40 @@ def tile_tftdictblock_pa_kernel(
         def emit_xn():
             j = k["n"]
             s, mv, rstd = x_t[("s", j)]
-            xh = xpool.tile([P, D], F32, name="xh", tag="xh", bufs=2)
+            xh = xpool.tile([P, D], F32, name="xh", tag="xh", bufs=4)
             nc.vector.tensor_scalar(
                 out=xh[:], in0=s[:], scalar1=mv[:, 0:1], scalar2=rstd[:], op0=ALU.subtract, op1=ALU.mult
             )
-            xps = ps_fc.tile([P, 4, P], F32, name="xps", tag="fc")
             for t in range(4):
-                nc.tensor.transpose(xps[:, t, :], xh[:, P * t : P * (t + 1)], ident_f[:])
-            x_t[("ps", j)] = xps
+                if j == 0:
+                    xps = ps_fc.tile([P, T], F32, name="xps", tag="fc")
+                    x_t[("ps", t)] = xps
+                nc.tensor.transpose(x_t[("ps", t)][:, P * j : P * (j + 1)], xh[:, P * t : P * (t + 1)], ident_f[:])
             k["n"] += 1
 
         def emit_xc(on_vector):
-            j = k["x"]
-            xps = x_t[("ps", j)]
-            for t in range(4):
-                dst = x2p[:, t, P * j : P * (j + 1)]
-                if on_vector:
-                    nc.vector.tensor_scalar(
-                        out=dst, in0=xps[:, t, :], scalar1=cols[:, t, 0:1], scalar2=cols[:, t, 1:2],
-                        op0=ALU.mult, op1=ALU.add,
-                    )
-                else:
-                    nc.scalar.activation(
-                        out=dst, in_=xps[:, t, :], func=ACT.Identity, bias=cols[:, t, 1:2], scale=cols[:, t, 0:1]
-                    )
+            t = k["x"]
+            xps = x_t[("ps", t)]
+            if on_vector:
+                nc.vector.tensor_scalar(
+                    out=x2p[:, t, :], in0=xps[:], scalar1=cols[:, t, 0:1], scalar2=cols[:, t, 1:2],
+                    op0=ALU.mult, op1=ALU.add,
+                )
+            else:
+                nc.scalar.activation(
+                    out=x2p[:, t, :], in_=xps[:], func=ACT.Identity, bias=cols[:, t, 1:2], scale=cols[:, t, 0:1]
+                )
             k["x"] += 1
 
         def emit_xr():
-            j = k["r"]
-            ns = slice(P * j, P * (j + 1))
             nc.vector.tensor_copy(
-                out=x2g[:, ns, :].rearrange("p (n i) t -> p n t i", i=4),
-                in_=x2p[:, :, ns].rearrange("p t (n i) -> p n t i", i=4),
+                out=x2g[:].rearrange("p (n i) t -> p n t i", i=4),
+                in_=x2p[:].rearrange("p t (n i) -> p n t i", i=4),
             )
             k["r"] += 1
 
         def emit_qx():
-            j = k["Q"]
-            ns = slice(P * j, P * (j + 1))
-            nc.vector.quantize_mx(
-                out=xc[:, ns].bitcast(FP8X4), scales=xs[:, ns], in_=x2g[:, ns, :].rearrange("p n t -> p (n t)")
-            )
+            nc.vector.quantize_mx(out=xc[:].bitcast(FP8X4), scales=xs[:], in_=x2g[:].rearrange("p n t -> p (n t)"))
             k["Q"] += 1
 
         for tk in PROG:
@@ -444,6 +438,8 @@ def tile_tftdictblock_pa_kernel(
                 emit_xr()
             elif tk == "Q":
                 emit_qx()
+            elif tk == "e":
+                emit_e()
             elif tk == "f":
                 nc.vector.tensor_copy(out=cols[:], in_=cols_ps[:, :, 0:24])
         assert k["g"] == len(gelus) and k["4"] == len(head_pieces) and k["C"] == 40 and k["q"] == 20

@@ -22,12 +22,14 @@ NJ = T // P
 NC = FF // 512
 FLOPS = 2 * T * D * FF * H + 2 * T * FF * HD * H
 
-PROG = "!eaaaannnnfsvsvrQccqccqccqccqccqggggcCcggggRqGcCcggggRqGqcCcggggRqGcCcggggRqGqcCcggggRqGcCcPggggRqGqcc12ggggRqGcc34ggggRqGccggggRqGccPggggRqGcc12ggggRqGcc34ggggRqGggggRGPggggRG12ggggRG34ggggRGPRG12P312434"
 NTR = 3
 NFC = 4
+NPJ = 1
 PJ_POS = {6: 0, 11: 1, 16: 2, 19: 3}
-TAPER = True
 BC_AFTER = 13
+PRELUDE = 9
+COPIES = [1, 3, 3, 3, 3, 3, 3, 2, 2, 2, 2, 2, 2, 0, 0, 0]
+VCOPY = [0, 1, 1, 1, 1, 1, 1, 1, 1, 1, 1, 1, 1, 0, 0, 0]
 
 
 def tile_tftdictblock_pa_kernel(
@@ -39,16 +41,17 @@ def tile_tftdictblock_pa_kernel(
         xpool = ctx.enter_context(tc.tile_pool(name="xpool", bufs=1))
         small = ctx.enter_context(tc.tile_pool(name="small", bufs=4))
         rawp = ctx.enter_context(tc.tile_pool(name="rawp", bufs=12))
-        wgp = ctx.enter_context(tc.tile_pool(name="wgp", bufs=8))
+        wgp = ctx.enter_context(tc.tile_pool(name="wgp", bufs=9))
         wcp = ctx.enter_context(tc.tile_pool(name="wcp", bufs=12))
         pcp = ctx.enter_context(tc.tile_pool(name="pcp", bufs=4))
         gpp = ctx.enter_context(tc.tile_pool(name="gpp", bufs=3))
         ggp = ctx.enter_context(tc.tile_pool(name="ggp", bufs=2))
         gcp = ctx.enter_context(tc.tile_pool(name="gcp", bufs=8))
         fin = ctx.enter_context(tc.tile_pool(name="fin", bufs=2))
+        tail = ctx.enter_context(tc.tile_pool(name="tail", bufs=3))
         ps_tr = ctx.enter_context(tc.psum_pool(name="ps_tr", bufs=NTR))
         ps_fc = ctx.enter_context(tc.psum_pool(name="ps_fc", bufs=NFC))
-        ps_pj = ctx.enter_context(tc.psum_pool(name="ps_pj", bufs=1))
+        ps_pj = ctx.enter_context(tc.psum_pool(name="ps_pj", bufs=NPJ))
 
         units = []
         quad = 0
@@ -67,18 +70,23 @@ def tile_tftdictblock_pa_kernel(
                 unit_of_head[idx] = pos
 
         vec_a = const.tile([P, 512], BF16, name="vec_a")
-        nc.vector.memset(vec_a[:], 0.0)
+        nc.gpsimd.memset(vec_a[:], 0.0)
         nc.scalar.dma_start(out=vec_a[0:1, :], in_=ln2_w.rearrange("(o d) -> o d", o=1))
         nc.scalar.dma_start(out=vec_a[1:2, :], in_=ln2_b.rearrange("(o d) -> o d", o=1))
         nc.scalar.dma_start(out=vec_a[8:24, :], in_=fc_b.rearrange("h (c x) -> (h c) x", x=512))
+        nc.scalar.dma_start(out=vec_a[24:28, 0:P], in_=proj_b)
         warm_in = const.tile([P, 1], F32, name="warm_in")
         warm_out = const.tile([P, 1], F32, name="warm_out")
         nc.vector.memset(warm_in[:], 0.0)
         nc.scalar.activation(out=warm_out[:], in_=warm_in[:], func=ACT.Gelu)
-        neg_half1 = const.tile([P, 1], F32, name="neg_half1")
-        neg_half4 = const.tile([P, NJ, 1], F32, name="neg_half4")
-        nc.vector.memset(neg_half1[:], -0.5)
+        neg_half4 = const.tile([P, NJ], F32, name="neg_half4")
+        inv_col = const.tile([P, 1], F32, name="inv_col")
+        nc.vector.memset(inv_col[:], 1.0 / HD)
         nc.vector.memset(neg_half4[:], -0.5)
+        eps_col = const.tile([P, 1], F32, name="eps_col")
+        nc.vector.tensor_scalar(
+            out=eps_col[:], in0=warm_in[:], scalar1=EPS, scalar2=None, op0=ALU.add
+        )
         ident_bf = const.tile([P, P], BF16, name="ident_bf")
         ident_f = const.tile([P, P], F32, name="ident_f")
         make_identity(nc, ident_bf[:])
@@ -115,147 +123,103 @@ def tile_tftdictblock_pa_kernel(
         for pos in range(1, 20):
             load_unit(pos)
             if pos == BC_AFTER:
-                for r, vec in enumerate((proj_b, dln_w, dln_b)):
+                for r, vec in enumerate((dln_w, dln_b)):
                     bc = const.tile([P, 512], BF16, name="bc%d" % r)
                     nc.sync.dma_start(out=bc[:], in_=vec.rearrange("h d -> (h d)").partition_broadcast(P))
                     tail_bc.append(bc)
-        pb_bc, dw_bc, db_bc = tail_bc
+        dw_bc, db_bc = tail_bc
+        pb_bc = const.tile([P, HD], BF16, name="pb_bc")
+        nc.sync.dma_start(out=pb_bc[:], in_=proj_b[H - 1, :].partition_broadcast(P))
 
-        vec_a2 = const.tile([P, 512], BF16, name="vec_a2")
-        cols_ps = ps_pj.tile([P, 4, P], BF16, name="cols_ps", tag="pj")
-        cols = const.tile([P, 4, 24], F32, name="cols")
-
-        def emit_e():
-            nc.vector.tensor_copy(
-                out=vec_a2[:].rearrange("p (u e q) -> p u e q", u=2, e=2),
-                in_=vec_a[:].rearrange("p (u q e) -> p u e q", u=2, e=2),
-            )
-            for t in range(4):
-                nc.tensor.transpose(cols_ps[:, t, :], vec_a2[:, P * t : P * (t + 1)], ident_bf[:])
+        cols_ps = ps_pj.tile([P, 5, P], BF16, name="cols_ps", tag="pj")
+        cols = const.tile([P, 5, 28], F32, name="cols")
+        for t in range(4):
+            u, e = divmod(t, 2)
+            nc.tensor.transpose(cols_ps[:, t, :], vec_a[:, 256 * u + e : 256 * (u + 1) : 2], ident_bf[:])
+        nc.tensor.transpose(cols_ps[:, 4, :], vec_a[:, 0:P], ident_bf[:])
+        nc.vector.tensor_copy(out=cols[:], in_=cols_ps[:, :, 0:28])
 
         x2p = xpool.tile([P, 4, T], BF16, name="x2p")
         x2g = xpool.tile([P, T, 4], BF16, name="x2g", align_bytes=64)
         xc = xpool.tile([P, T], U32, name="xc", align_bytes=64)
         xs = xpool.tile([P, T], U8, name="xs", align_bytes=64)
 
-        gelus = []
-        rg_pieces = []
-        for r in range(16):
-            if TAPER and r == 15:
-                for half in range(2):
-                    for t in range(4):
-                        gelus.append((r, t, 2 * half, 2 * half + 2))
-                rg_pieces.append((r, 0, 2))
-                rg_pieces.append((r, 2, 4))
-            else:
-                for t in range(4):
-                    gelus.append((r, t, 0, 4))
-                rg_pieces.append((r, 0, 4))
-        head_pieces = []
-        for h in range(H):
-            if TAPER and h == H - 1:
-                head_pieces.append((h, 0, 2))
-                head_pieces.append((h, 2, 4))
-            else:
-                head_pieces.append((h, 0, 4))
+        tr_t = []
+        wg_t = []
+        w_ops = []
+        k = {"copies": 0, "fc": 0}
 
-        k = {}
-        for key in "TCqFgRGPanxrQ1234!":
-            k[key] = 0
-        tr_t = {}
-        wg_t = {}
-        w_ops = {}
-        a_t = {}
-        gp_t = {}
-        gg_t = {}
-        g_ops = {}
-        x_t = {}
-        ln_t = {}
-
-        def emit_t():
-            u, b = divmod(k["T"], 2)
+        def transpose_block():
+            u, b = divmod(len(tr_t), 2)
             raw32 = raws[u][:].bitcast(F32)
             tr = ps_tr.tile([P, 512], F32, name="tr", tag="tr")
             for q in range(4):
                 blk = 4 * b + q
                 nc.tensor.transpose(tr[:, P * q : P * (q + 1)], raw32[:, P * blk : P * (blk + 1)], ident_f[:])
-            tr_t[(u, b)] = tr
-            k["T"] += 1
+            tr_t.append(tr)
 
-        def ahead():
-            while k["!"] > 0 and k["T"] < min(k["C"] + NTR, 40):
-                emit_t()
+        def transposes_ahead():
+            while len(tr_t) < min(k["copies"] + NTR, 40):
+                transpose_block()
 
-        def emit_c(on_vector):
-            u, b = divmod(k["C"], 2)
-            while k["T"] <= k["C"]:
-                emit_t()
+        def copy_block(on_vector):
+            u, b = divmod(k["copies"], 2)
             if b == 0:
                 wg = wgp.tile([P, 2048], BF16, name="wg", tag="wg", align_bytes=64)
-                wg_t[u] = wg
+                wg_t.append(wg)
             dst = wg_t[u][:].bitcast(F32)[:, 512 * b : 512 * (b + 1)].rearrange("p (i f u) -> p i f u", i=2, u=2)
-            src = tr_t[(u, b)][:].rearrange("p (i u f) -> p i f u", i=2, u=2)
+            src = tr_t[k["copies"]][:].rearrange("p (i u f) -> p i f u", i=2, u=2)
             if on_vector:
                 nc.vector.tensor_copy(out=dst, in_=src)
             else:
                 nc.scalar.copy(out=dst, in_=src)
-            k["C"] += 1
-            ahead()
+            k["copies"] += 1
+            transposes_ahead()
 
-        def emit_qw():
-            u = k["q"]
+        def quantise_ready_unit():
+            u = len(w_ops)
+            if 2 * (u + 1) > k["copies"]:
+                return
             pool = wcp if units[u][0] == "fc" else pcp
             codes = pool.tile([P, 512], U32, name="codes", tag="codes", align_bytes=64)
             scales = pool.tile([P, 512], U8, name="scales", tag="scales", align_bytes=64)
             nc.vector.quantize_mx(out=codes[:].bitcast(FP8X4), scales=scales[:], in_=wg_t[u][:])
-            w_ops[u] = (codes, scales)
-            k["q"] += 1
+            w_ops.append((codes, scales))
 
-        def can_f():
-            if k["F"] >= 64 or k["Q"] < 1:
-                return False
-            if unit_of_quad[k["F"] // 4] >= k["q"]:
-                return False
-            return k["F"] < done_gelus() + NFC
+        a_t = {}
+        gp_t = {}
+        gg_t = {}
+        g_ops = {}
 
-        def done_gelus():
-            n = 0
-            for r, t, j0, j1 in gelus[: k["g"]]:
-                if j1 == NJ:
-                    n += 1
-            return n
+        def first_matmuls_ahead(done):
+            while k["fc"] < min(done + NFC, 64) and unit_of_quad[k["fc"] // 4] < len(w_ops):
+                r, t = divmod(k["fc"], 4)
+                wc, ws = w_ops[unit_of_quad[r]]
+                a_ps = ps_fc.tile([P, T], F32, name="a_ps", tag="fc")
+                cs = slice(P * t, P * (t + 1))
+                nc.tensor.matmul_mx(
+                    out=a_ps[:], lhsT=wc[:, cs].bitcast(FP8X4), lhsT_scale=ws[:, cs],
+                    rhs=xc[:].bitcast(FP8X4), rhs_scale=xs[:], start=True, stop=True,
+                )
+                a_t[(r, t)] = a_ps
+                k["fc"] += 1
 
-        def emit_f():
-            r, t = divmod(k["F"], 4)
-            wc, ws = w_ops[unit_of_quad[r]]
-            a_ps = ps_fc.tile([P, T], F32, name="a_ps", tag="fc")
-            cs = slice(P * t, P * (t + 1))
-            nc.tensor.matmul_mx(
-                out=a_ps[:], lhsT=wc[:, cs].bitcast(FP8X4), lhsT_scale=ws[:, cs],
-                rhs=xc[:].bitcast(FP8X4), rhs_scale=xs[:], start=True, stop=True,
-            )
-            a_t[(r, t)] = a_ps
-            k["F"] += 1
-
-        def emit_g():
-            r, t, j0, j1 = gelus[k["g"]]
-            while (r, t) not in a_t:
-                emit_f()
-            if r not in gp_t:
+        def gelus(r, j0, j1):
+            if j0 == 0:
                 gp = gpp.tile([P, 4, T], BF16, name="gp", tag="gp")
                 gp_t[r] = gp
             ns = slice(P * j0, P * j1)
-            nc.scalar.activation(
-                out=gp_t[r][:, t, ns], in_=a_t[(r, t)][:, ns], func=ACT.Gelu,
-                bias=cols[:, t, 8 + r : 9 + r], scale=1.0,
-            )
-            k["g"] += 1
-            while can_f():
-                emit_f()
+            for t in range(4):
+                first_matmuls_ahead(4 * r + t)
+                nc.scalar.activation(
+                    out=gp_t[r][:, t, ns], in_=a_t[(r, t)][:, ns], func=ACT.Gelu,
+                    bias=cols[:, t, 8 + r : 9 + r], scale=1.0,
+                )
+                if j1 == NJ:
+                    first_matmuls_ahead(4 * r + t + 1)
 
-        def emit_rg():
-            r, j0, j1 = rg_pieces[k["R"]]
-            if r not in gg_t:
+        def regroup(r, j0, j1):
+            if j0 == 0:
                 gg = ggp.tile([P, T, 4], BF16, name="gg", tag="gg", align_bytes=64)
                 gg_t[r] = gg
             ns = slice(P * j0, P * j1)
@@ -263,11 +227,9 @@ def tile_tftdictblock_pa_kernel(
                 out=gg_t[r][:, ns, :].rearrange("p (n i) t -> p n t i", i=4),
                 in_=gp_t[r][:, :, ns].rearrange("p t (n i) -> p n t i", i=4),
             )
-            k["R"] += 1
 
-        def emit_qg():
-            r, j0, j1 = rg_pieces[k["G"]]
-            if r not in g_ops:
+        def quantise_g(r, j0, j1):
+            if j0 == 0:
                 gc = gcp.tile([P, T], U32, name="gc", tag="gc", align_bytes=64)
                 gs = gcp.tile([P, T], U8, name="gs", tag="gs", align_bytes=64)
                 g_ops[r] = (gc, gs)
@@ -277,15 +239,71 @@ def tile_tftdictblock_pa_kernel(
                 out=gc[:, ns].bitcast(FP8X4), scales=gs[:, ns],
                 in_=gg_t[r][:, ns, :].rearrange("p n t -> p (n t)"),
             )
-            k["G"] += 1
 
-        def emit_p():
-            h, j0, j1 = head_pieces[k["P"]]
+        ln_t = {}
+        cmat = const.tile([P, HD], F32, name="cmat")
+        cdw = const.tile([P, H, HD], F32, name="cdw")
+
+        def second_matmul(h):
             pc, pscale = w_ops[unit_of_head[h]]
-            if j0 == 0:
-                p_ps = ps_pj.tile([P, j1 - j0, HD], F32, name="p_ps", tag="pj")
-            else:
-                p_ps = ps_tr.tile([P, j1 - j0, HD], F32, name="p_ps2", tag="tr")
+            pt_ps = ps_pj.tile([P, T], F32, name="pt_ps", tag="pj")
+            for c in range(NC):
+                gc, gs = g_ops[NC * h + c]
+                nc.tensor.matmul_mx(
+                    out=pt_ps[:],
+                    lhsT=pc[:, P * c : P * (c + 1)].bitcast(FP8X4), lhsT_scale=pscale[:, P * c : P * (c + 1)],
+                    rhs=gc[:].bitcast(FP8X4), rhs_scale=gs[:],
+                    start=(c == 0), stop=(c == NC - 1),
+                )
+            pt = fin.tile([P, T], F32, name="pt", tag="pt")
+            nc.scalar.activation(
+                out=pt[:], in_=pt_ps[:], func=ACT.Identity, bias=cols[:, 4, 24 + h : 25 + h], scale=1.0
+            )
+            ln_t[h] = {"pt": pt}
+
+        def centre(h):
+            ct_ps = ps_pj.tile([P, T], F32, name="ct_ps", tag="pj")
+            nc.tensor.matmul(ct_ps[:], cmat[:], ln_t[h]["pt"][:], start=True, stop=True)
+            sq = fin.tile([P, T], F32, name="sq", tag="sq")
+            nc.scalar.activation(out=sq[:], in_=ct_ps[:], func=ACT.Square)
+            ln_t[h]["sq"] = sq
+
+        def variance(h):
+            vs_ps = ps_pj.tile([P, NJ], F32, name="vs_ps", tag="pj")
+            for j in range(NJ):
+                nc.tensor.matmul(
+                    vs_ps[:, j : j + 1], ln_t[h]["sq"][:, P * j : P * (j + 1)], inv_col[:], start=True, stop=True
+                )
+            ve = small.tile([P, NJ], F32, name="ve", tag="ve")
+            nc.vector.tensor_scalar(out=ve[:], in0=vs_ps[:], scalar1=EPS, scalar2=None, op0=ALU.add)
+            rs = small.tile([P, NJ], F32, name="rs", tag="rs")
+            nc.gpsimd.tensor_tensor(out=rs[:], in0=ve[:], in1=neg_half4[:], op=ALU.pow)
+            ln_t[h]["rs"] = rs
+
+        def centred_gain(h):
+            cw_ps = ps_pj.tile([P, NJ, HD], F32, name="cw_ps", tag="pj")
+            for j in range(NJ):
+                nc.tensor.matmul(
+                    cw_ps[:, j, :], ln_t[h]["pt"][:, P * j : P * (j + 1)], cdw[:, h, :], start=True, stop=True
+                )
+            ln_t[h]["cw"] = cw_ps
+
+        def finish(h):
+            s = ln_t[h]
+            o = fin.tile([P, NJ, HD], F32, name="o", tag="o")
+            for j in range(NJ):
+                nc.vector.scalar_tensor_tensor(
+                    out=o[:, j, :], in0=s["cw"][:, j, :], scalar=s["rs"][:, j : j + 1],
+                    in1=db_bc[:, HD * h : HD * (h + 1)], op0=ALU.mult, op1=ALU.add,
+                )
+            nc.sync.dma_start(out=out[0, h].rearrange("(p j) d -> p j d", j=NJ), in_=o[:])
+
+        def last_head(j0, j1):
+            h = H - 1
+            pc, pscale = w_ops[unit_of_head[h]]
+            n = j1 - j0
+            hd = slice(HD * h, HD * (h + 1))
+            p_ps = ps_tr.tile([P, n, HD], F32, name="p_ps", tag="tr")
             for j in range(j0, j1):
                 for c in range(NC):
                     gc, gs = g_ops[NC * h + c]
@@ -295,151 +313,146 @@ def tile_tftdictblock_pa_kernel(
                         rhs=pc[:, P * c : P * (c + 1)].bitcast(FP8X4), rhs_scale=pscale[:, P * c : P * (c + 1)],
                         start=(c == 0), stop=(c == NC - 1),
                     )
-            ln_t[("p", k["P"])] = p_ps
-            k["P"] += 1
-
-        def emit_ln(stage):
-            i = k[stage]
-            h, j0, j1 = head_pieces[i]
-            n = j1 - j0
-            hd = slice(HD * h, HD * (h + 1))
-            if stage == "1":
-                pb = fin.tile([P, n, HD], F32, name="pb", tag="pb")
-                nc.vector.tensor_tensor(
-                    out=pb[:], in0=ln_t[("p", i)][:], in1=pb_bc[:, hd].unsqueeze(1).to_broadcast([P, n, HD]), op=ALU.add
-                )
-                ln_t[("pb", i)] = pb
-            elif stage == "2":
-                pb = ln_t[("pb", i)]
-                st4 = small.tile([P, n, 6], F32, name="st4", tag="st4")
-                mv4 = small.tile([P, n, 2], F32, name="mv4", tag="mv4")
-                for j in range(n):
-                    nc.vector.bn_stats(out=st4[:, j, :], in_=pb[:, j, :])
-                for j in range(n):
-                    nc.vector.bn_aggr(out=mv4[:, j, :], in_=st4[:, j, :])
-                ve4 = small.tile([P, n, 1], F32, name="ve4", tag="ve4")
-                nc.vector.tensor_scalar(out=ve4[:], in0=mv4[:, :, 1:2], scalar1=EPS, scalar2=None, op0=ALU.add)
-                rs4 = small.tile([P, n, 1], F32, name="rs4", tag="rs4")
-                nc.gpsimd.tensor_tensor(out=rs4[:], in0=ve4[:], in1=neg_half4[:, 0:n, :], op=ALU.pow)
-                ln_t[("mv", i)] = mv4
-                ln_t[("rs", i)] = rs4
-            elif stage == "3":
-                pb = ln_t[("pb", i)]
-                mv4 = ln_t[("mv", i)]
-                t1 = fin.tile([P, n, HD], F32, name="t1", tag="t1")
-                for j in range(n):
-                    nc.vector.scalar_tensor_tensor(
-                        out=t1[:, j, :], in0=pb[:, j, :], scalar=mv4[:, j, 0:1], in1=dw_bc[:, hd],
-                        op0=ALU.subtract, op1=ALU.mult,
-                    )
-                ln_t[("t1", i)] = t1
-            else:
-                t1 = ln_t[("t1", i)]
-                rs4 = ln_t[("rs", i)]
-                o = fin.tile([P, n, HD], F32, name="o", tag="o")
-                for j in range(n):
-                    nc.vector.scalar_tensor_tensor(
-                        out=o[:, j, :], in0=t1[:, j, :], scalar=rs4[:, j, :], in1=db_bc[:, hd],
-                        op0=ALU.mult, op1=ALU.add,
-                    )
-                nc.sync.dma_start(out=out[0, h].rearrange("(p j) d -> p j d", j=NJ)[:, j0:j1, :], in_=o[:])
-            k[stage] += 1
-
-        def emit_xa():
-            j = k["a"]
-            s = xpool.tile([P, D], F32, name="s", tag="s", bufs=4)
+            pb = tail.tile([P, n, HD], F32, name="pb", tag="pb")
             nc.vector.tensor_tensor(
-                out=s[:].rearrange("p (u e q) -> p u e q", u=2, e=2),
-                in0=xt_sb[:, j, :].rearrange("p (u q e) -> p u e q", u=2, e=2),
-                in1=xe_sb[:, j, :].rearrange("p (u q e) -> p u e q", u=2, e=2),
-                op=ALU.add,
+                out=pb[:], in0=p_ps[:], in1=pb_bc[:].unsqueeze(1).to_broadcast([P, n, HD]), op=ALU.add
             )
-            st = small.tile([P, 6], F32, name="st", tag="st")
-            nc.vector.bn_stats(out=st[:], in_=s[:])
-            mv = small.tile([P, 2], F32, name="mv", tag="mv")
-            nc.vector.bn_aggr(out=mv[:], in_=st[:])
-            ve = small.tile([P, 1], F32, name="ve", tag="ve")
-            nc.vector.tensor_scalar(out=ve[:], in0=mv[:, 1:2], scalar1=EPS, scalar2=None, op0=ALU.add)
-            rstd = small.tile([P, 1], F32, name="rstd", tag="rstd")
-            nc.gpsimd.tensor_tensor(out=rstd[:], in0=ve[:], in1=neg_half1[:], op=ALU.pow)
-            x_t[("s", j)] = (s, mv, rstd)
-            k["a"] += 1
+            st4 = small.tile([P, n, 6], F32, name="st4", tag="st4")
+            mv4 = small.tile([P, n, 2], F32, name="mv4", tag="mv4")
+            for j in range(n):
+                nc.vector.bn_stats(out=st4[:, j, :], in_=pb[:, j, :])
+            for j in range(n):
+                nc.vector.bn_aggr(out=mv4[:, j, :], in_=st4[:, j, :])
+            rs4 = small.tile([P, n, 1], F32, name="rs4", tag="rs4")
+            nc.scalar.activation(
+                out=rs4[:], in_=mv4[:, :, 1:2], func=ACT.Abs_reciprocal_sqrt, bias=eps_col[:], scale=1.0
+            )
+            t1 = tail.tile([P, n, HD], F32, name="t1", tag="t1")
+            for j in range(n):
+                nc.vector.scalar_tensor_tensor(
+                    out=t1[:, j, :], in0=pb[:, j, :], scalar=mv4[:, j, 0:1], in1=dw_bc[:, hd],
+                    op0=ALU.subtract, op1=ALU.mult,
+                )
+            o = tail.tile([P, n, HD], F32, name="o3", tag="o3")
+            for j in range(n):
+                nc.vector.scalar_tensor_tensor(
+                    out=o[:, j, :], in0=t1[:, j, :], scalar=rs4[:, j, :], in1=db_bc[:, hd],
+                    op0=ALU.mult, op1=ALU.add,
+                )
+            nc.sync.dma_start(out=out[0, h].rearrange("(p j) d -> p j d", j=NJ)[:, j0:j1, :], in_=o[:])
 
-        def emit_xn():
-            j = k["n"]
-            s, mv, rstd = x_t[("s", j)]
+        transposes_ahead()
+        norm = []
+        xsum = const.tile([P, NJ], F32, name="xsum")
+        xnm = const.tile([P, NJ], F32, name="xnm")
+        xss = const.tile([P, NJ], F32, name="xss")
+        xve = const.tile([P, NJ], F32, name="xve")
+        xrs = const.tile([P, NJ], F32, name="xrs")
+        for j in range(NJ):
+            s = xpool.tile([P, D], F32, name="s", tag="s", bufs=4)
+            nc.vector.scalar_tensor_tensor(
+                out=s[:], in0=xt_sb[:, j, :], scalar=1.0, in1=xe_sb[:, j, :], op0=ALU.mult, op1=ALU.add,
+                accum_out=xsum[:, j : j + 1],
+            )
+            nc.vector.tensor_scalar(
+                out=xnm[:, j : j + 1], in0=xsum[:, j : j + 1], scalar1=-1.0 / D, scalar2=None, op0=ALU.mult
+            )
+            sq = xpool.tile([P, D], F32, name="xsq", tag="xsq", bufs=2)
+            nc.scalar.activation(
+                out=sq[:], in_=s[:], func=ACT.Square, bias=xnm[:, j : j + 1], scale=1.0, accum_out=xss[:, j : j + 1]
+            )
+            norm.append(s)
+            if j % 2:
+                js = slice(j - 1, j + 1)
+                nc.vector.tensor_scalar(
+                    out=xve[:, js], in0=xss[:, js], scalar1=1.0 / D, scalar2=EPS, op0=ALU.mult, op1=ALU.add
+                )
+                nc.gpsimd.tensor_tensor(out=xrs[:, js], in0=xve[:, js], in1=neg_half4[:, js], op=ALU.pow)
+        copy_block(False)
+        copy_block(False)
+        quantise_ready_unit()
+        xps_t = []
+        for j in range(NJ):
+            if j == 2:
+                copy_block(False)
+                copy_block(False)
+            s = norm[j]
             xh = xpool.tile([P, D], F32, name="xh", tag="xh", bufs=4)
             nc.vector.tensor_scalar(
-                out=xh[:], in0=s[:], scalar1=mv[:, 0:1], scalar2=rstd[:], op0=ALU.subtract, op1=ALU.mult
+                out=xh[:].rearrange("p (u e q) -> p u e q", u=2, e=2),
+                in0=s[:].rearrange("p (u q e) -> p u e q", u=2, e=2),
+                scalar1=xnm[:, j : j + 1], scalar2=xrs[:, j : j + 1], op0=ALU.add, op1=ALU.mult,
             )
             for t in range(4):
                 if j == 0:
                     xps = ps_fc.tile([P, T], F32, name="xps", tag="fc")
-                    x_t[("ps", t)] = xps
-                nc.tensor.transpose(x_t[("ps", t)][:, P * j : P * (j + 1)], xh[:, P * t : P * (t + 1)], ident_f[:])
-            k["n"] += 1
-
-        def emit_xc(on_vector):
-            t = k["x"]
-            xps = x_t[("ps", t)]
-            if on_vector:
+                    xps_t.append(xps)
+                nc.tensor.transpose(xps_t[t][:, P * j : P * (j + 1)], xh[:, P * t : P * (t + 1)], ident_f[:])
+        for t in range(4):
+            if t % 2:
                 nc.vector.tensor_scalar(
-                    out=x2p[:, t, :], in0=xps[:], scalar1=cols[:, t, 0:1], scalar2=cols[:, t, 1:2],
+                    out=x2p[:, t, :], in0=xps_t[t][:], scalar1=cols[:, t, 0:1], scalar2=cols[:, t, 1:2],
                     op0=ALU.mult, op1=ALU.add,
                 )
             else:
                 nc.scalar.activation(
-                    out=x2p[:, t, :], in_=xps[:], func=ACT.Identity, bias=cols[:, t, 1:2], scale=cols[:, t, 0:1]
+                    out=x2p[:, t, :], in_=xps_t[t][:], func=ACT.Identity, bias=cols[:, t, 1:2], scale=cols[:, t, 0:1]
                 )
-            k["x"] += 1
+        quantise_ready_unit()
+        nc.vector.tensor_copy(
+            out=x2g[:].rearrange("p (n i) t -> p n t i", i=4),
+            in_=x2p[:].rearrange("p t (n i) -> p n t i", i=4),
+        )
+        nc.vector.quantize_mx(out=xc[:].bitcast(FP8X4), scales=xs[:], in_=x2g[:].rearrange("p n t -> p (n t)"))
 
-        def emit_xr():
-            nc.vector.tensor_copy(
-                out=x2g[:].rearrange("p (n i) t -> p n t i", i=4),
-                in_=x2p[:].rearrange("p t (n i) -> p n t i", i=4),
-            )
-            k["r"] += 1
+        nc.gpsimd.tensor_scalar(
+            out=cmat[:], in0=ident_f[:],
+            scalar1=1.0, scalar2=-1.0 / HD, op0=ALU.mult, op1=ALU.add,
+        )
+        nc.gpsimd.tensor_tensor(
+            out=cdw[:], in0=cmat[:].unsqueeze(1).to_broadcast([P, H, HD]),
+            in1=dw_bc[:].rearrange("p (h d) -> p h d", h=H), op=ALU.mult
+        )
 
-        def emit_qx():
-            nc.vector.quantize_mx(out=xc[:].bitcast(FP8X4), scales=xs[:], in_=x2g[:].rearrange("p n t -> p (n t)"))
-            k["Q"] += 1
+        while k["copies"] < PRELUDE:
+            copy_block(False)
+            quantise_ready_unit()
 
-        for tk in PROG:
-            if tk == "t":
-                emit_t()
-            elif tk == "!":
-                k["!"] = 1
-                ahead()
-            elif tk == "c":
-                emit_c(False)
-            elif tk == "C":
-                emit_c(True)
-            elif tk == "q":
-                emit_qw()
-            elif tk == "g":
-                emit_g()
-            elif tk == "R":
-                emit_rg()
-            elif tk == "G":
-                emit_qg()
-            elif tk == "P":
-                emit_p()
-            elif tk in "1234":
-                emit_ln(tk)
-            elif tk == "a":
-                emit_xa()
-            elif tk == "n":
-                emit_xn()
-            elif tk == "s":
-                emit_xc(False)
-            elif tk == "v":
-                emit_xc(True)
-            elif tk == "r":
-                emit_xr()
-            elif tk == "Q":
-                emit_qx()
-            elif tk == "e":
-                emit_e()
-            elif tk == "f":
-                nc.vector.tensor_copy(out=cols[:], in_=cols_ps[:, :, 0:24])
-        assert k["g"] == len(gelus) and k["4"] == len(head_pieces) and k["C"] == 40 and k["q"] == 20
+        for r in range(15):
+            for i in range(COPIES[r]):
+                copy_block(i == 0 and VCOPY[r] == 1)
+            h, step = divmod(r - 5, 4)
+            if h >= 0 and step == 0:
+                second_matmul(h)
+            if h >= 0 and step == 1:
+                variance(h)
+            gelus(r, 0, NJ)
+            if h >= 0 and step == 0:
+                centre(h)
+            if h >= 0 and step == 1:
+                centred_gain(h)
+            if r:
+                regroup(r - 1, 0, NJ)
+                quantise_ready_unit()
+                quantise_g(r - 1, 0, NJ)
+                quantise_ready_unit()
+            if h >= 0 and step == 2:
+                finish(h)
+        gelus(15, 0, 2)
+        regroup(14, 0, NJ)
+        finish(2)
+        quantise_g(14, 0, NJ)
+        for j0, j1, k0, k1 in ((2, 3, 0, 2), (3, 4, 2, 3)):
+            gelus(15, j0, j1)
+            regroup(15, k0, k1)
+            quantise_g(15, k0, k1)
+        table_out = const.tile([P, 1], F32, name="table_out")
+        nc.scalar.activation(
+            out=table_out[:], in_=gp_t[15][:, 3, T - 1 : T], func=ACT.Abs_reciprocal_sqrt, bias=1.0, scale=0.0
+        )
+        regroup(15, 3, 4)
+        quantise_g(15, 3, 4)
+        last_head(0, 2)
+        last_head(2, 3)
+        last_head(3, 4)
+        assert k["copies"] == 40 and len(w_ops) == 20 and k["fc"] == 64

@@ -1,4 +1,5 @@
 from contextlib import ExitStack
+from functools import partial
 
 import concourse.mybir as mybir
 from concourse.masks import make_identity
@@ -27,9 +28,8 @@ NFC = 4
 NPJ = 1
 PJ_POS = {6: 0, 11: 1, 16: 2, 19: 3}
 BC_AFTER = 13
-PRELUDE = 9
-COPIES = [1, 3, 3, 3, 3, 3, 3, 2, 2, 2, 2, 2, 2, 0, 0, 0]
-VCOPY = [0, 1, 1, 1, 1, 1, 1, 1, 1, 1, 1, 1, 1, 0, 0, 0]
+S_COPIES = [2, 1, 2, 1, 2, 1, 1, 1, 2, 1, 1, 1, 2, 0, 0]
+V_COPIES = [1, 1, 1, 1, 1, 1, 2, 1, 1, 1, 2, 1, 1, 0, 0]
 
 
 def tile_tftdictblock_pa_kernel(
@@ -99,8 +99,8 @@ def tile_tftdictblock_pa_kernel(
         raws = []
         tail_bc = []
 
-        def load_x(half):
-            js = slice(2 * half, 2 * half + 2)
+        def load_x(j0, j1):
+            js = slice(j0, j1)
             nc.sync.dma_start(out=xt_sb[:, js, :], in_=xt_v[:, js, :])
             nc.sync.dma_start(out=xe_sb[:, js, :], in_=xe_v[:, js, :])
 
@@ -117,9 +117,10 @@ def tile_tftdictblock_pa_kernel(
                 nc.sync.dma_start(out=raw[:], in_=proj_w[idx, :, :])
             raws.append(raw)
 
-        load_x(0)
+        load_x(0, 1)
+        load_x(1, 2)
+        load_x(2, 4)
         load_unit(0)
-        load_x(1)
         for pos in range(1, 20):
             load_unit(pos)
             if pos == BC_AFTER:
@@ -133,11 +134,6 @@ def tile_tftdictblock_pa_kernel(
 
         cols_ps = ps_pj.tile([P, 5, P], BF16, name="cols_ps", tag="pj")
         cols = const.tile([P, 5, 28], F32, name="cols")
-        for t in range(4):
-            u, e = divmod(t, 2)
-            nc.tensor.transpose(cols_ps[:, t, :], vec_a[:, 256 * u + e : 256 * (u + 1) : 2], ident_bf[:])
-        nc.tensor.transpose(cols_ps[:, 4, :], vec_a[:, 0:P], ident_bf[:])
-        nc.vector.tensor_copy(out=cols[:], in_=cols_ps[:, :, 0:28])
 
         x2p = xpool.tile([P, 4, T], BF16, name="x2p")
         x2g = xpool.tile([P, T, 4], BF16, name="x2g", align_bytes=64)
@@ -158,8 +154,8 @@ def tile_tftdictblock_pa_kernel(
                 nc.tensor.transpose(tr[:, P * q : P * (q + 1)], raw32[:, P * blk : P * (blk + 1)], ident_f[:])
             tr_t.append(tr)
 
-        def transposes_ahead():
-            while len(tr_t) < min(k["copies"] + NTR, 40):
+        def transposes_ahead(n):
+            while len(tr_t) < min(k["copies"] + n, 40):
                 transpose_block()
 
         def copy_block(on_vector):
@@ -174,7 +170,6 @@ def tile_tftdictblock_pa_kernel(
             else:
                 nc.scalar.copy(out=dst, in_=src)
             k["copies"] += 1
-            transposes_ahead()
 
         def quantise_ready_unit():
             u = len(w_ops)
@@ -204,12 +199,16 @@ def tile_tftdictblock_pa_kernel(
                 a_t[(r, t)] = a_ps
                 k["fc"] += 1
 
+        hooks = {}
+
         def gelus(r, j0, j1):
             if j0 == 0:
                 gp = gpp.tile([P, 4, T], BF16, name="gp", tag="gp")
                 gp_t[r] = gp
             ns = slice(P * j0, P * j1)
             for t in range(4):
+                if j0 == 0:
+                    hooks.get((r, t), lambda: None)()
                 first_matmuls_ahead(4 * r + t)
                 nc.scalar.activation(
                     out=gp_t[r][:, t, ns], in_=a_t[(r, t)][:, ns], func=ACT.Gelu,
@@ -255,17 +254,23 @@ def tile_tftdictblock_pa_kernel(
                     rhs=gc[:].bitcast(FP8X4), rhs_scale=gs[:],
                     start=(c == 0), stop=(c == NC - 1),
                 )
+            ln_t[h] = {"pt_ps": pt_ps}
+
+        def biased(h):
             pt = fin.tile([P, T], F32, name="pt", tag="pt")
             nc.scalar.activation(
-                out=pt[:], in_=pt_ps[:], func=ACT.Identity, bias=cols[:, 4, 24 + h : 25 + h], scale=1.0
+                out=pt[:], in_=ln_t[h]["pt_ps"][:], func=ACT.Identity, bias=cols[:, 4, 24 + h : 25 + h], scale=1.0
             )
-            ln_t[h] = {"pt": pt}
+            ln_t[h]["pt"] = pt
 
         def centre(h):
             ct_ps = ps_pj.tile([P, T], F32, name="ct_ps", tag="pj")
             nc.tensor.matmul(ct_ps[:], cmat[:], ln_t[h]["pt"][:], start=True, stop=True)
+            ln_t[h]["ct"] = ct_ps
+
+        def squared(h):
             sq = fin.tile([P, T], F32, name="sq", tag="sq")
-            nc.scalar.activation(out=sq[:], in_=ct_ps[:], func=ACT.Square)
+            nc.scalar.activation(out=sq[:], in_=ln_t[h]["ct"][:], func=ACT.Square)
             ln_t[h]["sq"] = sq
 
         def variance(h):
@@ -274,14 +279,20 @@ def tile_tftdictblock_pa_kernel(
                 nc.tensor.matmul(
                     vs_ps[:, j : j + 1], ln_t[h]["sq"][:, P * j : P * (j + 1)], inv_col[:], start=True, stop=True
                 )
+            ln_t[h]["vs"] = vs_ps
+
+        def rstd(h):
             ve = small.tile([P, NJ], F32, name="ve", tag="ve")
-            nc.vector.tensor_scalar(out=ve[:], in0=vs_ps[:], scalar1=EPS, scalar2=None, op0=ALU.add)
+            nc.vector.tensor_scalar(out=ve[:], in0=ln_t[h]["vs"][:], scalar1=EPS, scalar2=None, op0=ALU.add)
             rs = small.tile([P, NJ], F32, name="rs", tag="rs")
             nc.gpsimd.tensor_tensor(out=rs[:], in0=ve[:], in1=neg_half4[:], op=ALU.pow)
             ln_t[h]["rs"] = rs
 
         def centred_gain(h):
-            cw_ps = ps_pj.tile([P, NJ, HD], F32, name="cw_ps", tag="pj")
+            if h == H - 2:
+                cw_ps = ps_tr.tile([P, NJ, HD], F32, name="cw_ps2", tag="tr")
+            else:
+                cw_ps = ps_pj.tile([P, NJ, HD], F32, name="cw_ps", tag="pj")
             for j in range(NJ):
                 nc.tensor.matmul(
                     cw_ps[:, j, :], ln_t[h]["pt"][:, P * j : P * (j + 1)], cdw[:, h, :], start=True, stop=True
@@ -298,57 +309,130 @@ def tile_tftdictblock_pa_kernel(
                 )
             nc.sync.dma_start(out=out[0, h].rearrange("(p j) d -> p j d", j=NJ), in_=o[:])
 
-        def last_head(j0, j1):
-            h = H - 1
-            pc, pscale = w_ops[unit_of_head[h]]
+        last = {}
+        hd3 = slice(HD * (H - 1), HD * H)
+
+        def last_matmuls(j0, j1):
+            pc, pscale = w_ops[unit_of_head[H - 1]]
             n = j1 - j0
-            hd = slice(HD * h, HD * (h + 1))
             p_ps = ps_tr.tile([P, n, HD], F32, name="p_ps", tag="tr")
             for j in range(j0, j1):
                 for c in range(NC):
-                    gc, gs = g_ops[NC * h + c]
+                    gc, gs = g_ops[NC * (H - 1) + c]
                     nc.tensor.matmul_mx(
                         out=p_ps[:, j - j0, :],
                         lhsT=gc[:, P * j : P * (j + 1)].bitcast(FP8X4), lhsT_scale=gs[:, P * j : P * (j + 1)],
                         rhs=pc[:, P * c : P * (c + 1)].bitcast(FP8X4), rhs_scale=pscale[:, P * c : P * (c + 1)],
                         start=(c == 0), stop=(c == NC - 1),
                     )
+            last[j0] = {"n": n, "p": p_ps}
+
+        def last_biased(j0):
+            n = last[j0]["n"]
             pb = tail.tile([P, n, HD], F32, name="pb", tag="pb")
             nc.vector.tensor_tensor(
-                out=pb[:], in0=p_ps[:], in1=pb_bc[:].unsqueeze(1).to_broadcast([P, n, HD]), op=ALU.add
+                out=pb[:], in0=last[j0]["p"][:], in1=pb_bc[:].unsqueeze(1).to_broadcast([P, n, HD]), op=ALU.add
             )
-            st4 = small.tile([P, n, 6], F32, name="st4", tag="st4")
-            mv4 = small.tile([P, n, 2], F32, name="mv4", tag="mv4")
+            last[j0]["pb"] = pb
+
+        def last_stats(j0):
+            n = last[j0]["n"]
+            st4 = tail.tile([P, n, 6], F32, name="st4", tag="st4")
+            mv4 = tail.tile([P, n, 2], F32, name="mv4", tag="mv4")
             for j in range(n):
-                nc.vector.bn_stats(out=st4[:, j, :], in_=pb[:, j, :])
+                nc.vector.bn_stats(out=st4[:, j, :], in_=last[j0]["pb"][:, j, :])
             for j in range(n):
                 nc.vector.bn_aggr(out=mv4[:, j, :], in_=st4[:, j, :])
-            rs4 = small.tile([P, n, 1], F32, name="rs4", tag="rs4")
+            rs4 = tail.tile([P, n, 1], F32, name="rs4", tag="rs4")
             nc.scalar.activation(
                 out=rs4[:], in_=mv4[:, :, 1:2], func=ACT.Abs_reciprocal_sqrt, bias=eps_col[:], scale=1.0
             )
+            last[j0]["mv"] = mv4
+            last[j0]["rs"] = rs4
+
+        def last_gain(j0):
+            n = last[j0]["n"]
             t1 = tail.tile([P, n, HD], F32, name="t1", tag="t1")
             for j in range(n):
                 nc.vector.scalar_tensor_tensor(
-                    out=t1[:, j, :], in0=pb[:, j, :], scalar=mv4[:, j, 0:1], in1=dw_bc[:, hd],
+                    out=t1[:, j, :], in0=last[j0]["pb"][:, j, :], scalar=last[j0]["mv"][:, j, 0:1], in1=dw_bc[:, hd3],
                     op0=ALU.subtract, op1=ALU.mult,
                 )
+            last[j0]["t1"] = t1
+
+        def last_finish(j0):
+            n = last[j0]["n"]
             o = tail.tile([P, n, HD], F32, name="o3", tag="o3")
             for j in range(n):
                 nc.vector.scalar_tensor_tensor(
-                    out=o[:, j, :], in0=t1[:, j, :], scalar=rs4[:, j, :], in1=db_bc[:, hd],
+                    out=o[:, j, :], in0=last[j0]["t1"][:, j, :], scalar=last[j0]["rs"][:, j, :], in1=db_bc[:, hd3],
                     op0=ALU.mult, op1=ALU.add,
                 )
-            nc.sync.dma_start(out=out[0, h].rearrange("(p j) d -> p j d", j=NJ)[:, j0:j1, :], in_=o[:])
+            nc.sync.dma_start(out=out[0, H - 1].rearrange("(p j) d -> p j d", j=NJ)[:, j0 : j0 + n, :], in_=o[:])
 
-        transposes_ahead()
+        half = T // 2
+
+        def first_half():
+            h = H - 1
+            pc, pscale = w_ops[unit_of_head[h]]
+            pt_ps = ps_tr.tile([P, half], F32, name="pt_half_ps", tag="tr")
+            for c in range(NC):
+                gc, gs = g_ops[NC * h + c]
+                nc.tensor.matmul_mx(
+                    out=pt_ps[:],
+                    lhsT=pc[:, P * c : P * (c + 1)].bitcast(FP8X4), lhsT_scale=pscale[:, P * c : P * (c + 1)],
+                    rhs=gc[:, 0:half].bitcast(FP8X4), rhs_scale=gs[:, 0:half],
+                    start=(c == 0), stop=(c == NC - 1),
+                )
+            pt = tail.tile([P, half], F32, name="pt_half", tag="pt_half")
+            nc.scalar.activation(
+                out=pt[:], in_=pt_ps[:], func=ACT.Identity, bias=cols[:, 4, 24 + h : 25 + h], scale=1.0
+            )
+            last["pt"] = pt
+
+        def first_half_centre():
+            pt = last["pt"]
+            ct_ps = ps_pj.tile([P, half], F32, name="ct_half_ps", tag="pj")
+            nc.tensor.matmul(ct_ps[:], cmat[:], pt[:], start=True, stop=True)
+            sq = tail.tile([P, half], F32, name="sq_half", tag="sq_half")
+            nc.scalar.activation(out=sq[:], in_=ct_ps[:], func=ACT.Square)
+            last["sq"] = sq
+
+        def first_half_gain():
+            cw_ps = ps_tr.tile([P, 2, HD], F32, name="cw_half_ps", tag="tr")
+            vs_ps = ps_pj.tile([P, 2], F32, name="vs_half_ps", tag="pj")
+            for j in range(2):
+                nc.tensor.matmul(
+                    cw_ps[:, j, :], last["pt"][:, P * j : P * (j + 1)], cdw[:, H - 1, :], start=True, stop=True
+                )
+            for j in range(2):
+                nc.tensor.matmul(
+                    vs_ps[:, j : j + 1], last["sq"][:, P * j : P * (j + 1)], inv_col[:], start=True, stop=True
+                )
+            rs = tail.tile([P, 2], F32, name="rs_half", tag="rs_half")
+            nc.scalar.activation(
+                out=rs[:], in_=vs_ps[:], func=ACT.Abs_reciprocal_sqrt, bias=eps_col[:], scale=1.0
+            )
+            last["cw"] = cw_ps
+            last["rs"] = rs
+
+        def first_half_finish():
+            o = tail.tile([P, 2, HD], F32, name="o_half", tag="o3")
+            for j in range(2):
+                nc.vector.scalar_tensor_tensor(
+                    out=o[:, j, :], in0=last["cw"][:, j, :], scalar=last["rs"][:, j : j + 1], in1=db_bc[:, hd3],
+                    op0=ALU.mult, op1=ALU.add,
+                )
+            nc.sync.dma_start(out=out[0, H - 1].rearrange("(p j) d -> p j d", j=NJ)[:, 0:2, :], in_=o[:])
+
         norm = []
         xsum = const.tile([P, NJ], F32, name="xsum")
         xnm = const.tile([P, NJ], F32, name="xnm")
         xss = const.tile([P, NJ], F32, name="xss")
         xve = const.tile([P, NJ], F32, name="xve")
         xrs = const.tile([P, NJ], F32, name="xrs")
-        for j in range(NJ):
+
+        def x_add(j):
             s = xpool.tile([P, D], F32, name="s", tag="s", bufs=4)
             nc.vector.scalar_tensor_tensor(
                 out=s[:], in0=xt_sb[:, j, :], scalar=1.0, in1=xe_sb[:, j, :], op0=ALU.mult, op1=ALU.add,
@@ -362,20 +446,16 @@ def tile_tftdictblock_pa_kernel(
                 out=sq[:], in_=s[:], func=ACT.Square, bias=xnm[:, j : j + 1], scale=1.0, accum_out=xss[:, j : j + 1]
             )
             norm.append(s)
-            if j % 2:
-                js = slice(j - 1, j + 1)
-                nc.vector.tensor_scalar(
-                    out=xve[:, js], in0=xss[:, js], scalar1=1.0 / D, scalar2=EPS, op0=ALU.mult, op1=ALU.add
-                )
-                nc.gpsimd.tensor_tensor(out=xrs[:, js], in0=xve[:, js], in1=neg_half4[:, js], op=ALU.pow)
-        copy_block(False)
-        copy_block(False)
-        quantise_ready_unit()
+
+        def x_rstd(js):
+            nc.vector.tensor_scalar(
+                out=xve[:, js], in0=xss[:, js], scalar1=1.0 / D, scalar2=EPS, op0=ALU.mult, op1=ALU.add
+            )
+            nc.gpsimd.tensor_tensor(out=xrs[:, js], in0=xve[:, js], in1=neg_half4[:, js], op=ALU.pow)
+
         xps_t = []
-        for j in range(NJ):
-            if j == 2:
-                copy_block(False)
-                copy_block(False)
+
+        def x_norm(j):
             s = norm[j]
             xh = xpool.tile([P, D], F32, name="xh", tag="xh", bufs=4)
             nc.vector.tensor_scalar(
@@ -388,8 +468,9 @@ def tile_tftdictblock_pa_kernel(
                     xps = ps_fc.tile([P, T], F32, name="xps", tag="fc")
                     xps_t.append(xps)
                 nc.tensor.transpose(xps_t[t][:, P * j : P * (j + 1)], xh[:, P * t : P * (t + 1)], ident_f[:])
-        for t in range(4):
-            if t % 2:
+
+        def x_affine(t, on_vector):
+            if on_vector:
                 nc.vector.tensor_scalar(
                     out=x2p[:, t, :], in0=xps_t[t][:], scalar1=cols[:, t, 0:1], scalar2=cols[:, t, 1:2],
                     op0=ALU.mult, op1=ALU.add,
@@ -398,13 +479,47 @@ def tile_tftdictblock_pa_kernel(
                 nc.scalar.activation(
                     out=x2p[:, t, :], in_=xps_t[t][:], func=ACT.Identity, bias=cols[:, t, 1:2], scale=cols[:, t, 0:1]
                 )
+
+        def copies(n, on_vector):
+            for i in range(n):
+                if k["copies"] < 40:
+                    copy_block(on_vector)
+                    transposes_ahead(NTR)
+
+        ctx.enter_context(tc.manual_schedule())
+        transposes_ahead(2)
+        x_add(0)
+        x_add(1)
+        x_add(2)
+        x_rstd(slice(0, 2))
+        x_add(3)
+        for t in range(4):
+            u, e = divmod(t, 2)
+            nc.tensor.transpose(cols_ps[:, t, :], vec_a[:, 256 * u + e : 256 * (u + 1) : 2], ident_bf[:])
+        nc.tensor.transpose(cols_ps[:, 4, :], vec_a[:, 0:P], ident_bf[:])
+        transposes_ahead(NTR)
+        x_norm(0)
+        x_norm(1)
+        x_rstd(slice(2, 4))
+        nc.vector.tensor_copy(out=cols[:], in_=cols_ps[:, :, 0:28])
+        copies(1, False)
+        x_norm(2)
+        x_norm(3)
+        copies(2, False)
         quantise_ready_unit()
+        for t in range(4):
+            x_affine(t, t % 2 == 1)
         nc.vector.tensor_copy(
             out=x2g[:].rearrange("p (n i) t -> p n t i", i=4),
             in_=x2p[:].rearrange("p t (n i) -> p n t i", i=4),
         )
         nc.vector.quantize_mx(out=xc[:].bitcast(FP8X4), scales=xs[:], in_=x2g[:].rearrange("p n t -> p (n t)"))
-
+        copies(3, False)
+        copy_block(False)
+        quantise_ready_unit()
+        first_matmuls_ahead(0)
+        quantise_ready_unit()
+        transposes_ahead(NTR)
         nc.gpsimd.tensor_scalar(
             out=cmat[:], in0=ident_f[:],
             scalar1=1.0, scalar2=-1.0 / HD, op0=ALU.mult, op1=ALU.add,
@@ -414,45 +529,56 @@ def tile_tftdictblock_pa_kernel(
             in1=dw_bc[:].rearrange("p (h d) -> p h d", h=H), op=ALU.mult
         )
 
-        while k["copies"] < PRELUDE:
-            copy_block(False)
-            quantise_ready_unit()
+        for h in range(H - 1):
+            r = NC * h + 5
+            hooks[(r, 1)] = partial(second_matmul, h)
+            hooks[(r + 1, 0)] = partial(biased, h)
+            hooks[(r + 1, 1)] = partial(centre, h)
+            hooks[(r + 1, 3)] = partial(squared, h)
+            hooks[(r + 2, 0)] = partial(variance, h)
+            if h < H - 2:
+                hooks[(r + 2, 3)] = partial(centred_gain, h)
+            else:
+                hooks[(r + 1, 2)] = partial(centred_gain, h)
 
         for r in range(15):
-            for i in range(COPIES[r]):
-                copy_block(i == 0 and VCOPY[r] == 1)
-            h, step = divmod(r - 5, 4)
-            if h >= 0 and step == 0:
-                second_matmul(h)
-            if h >= 0 and step == 1:
-                variance(h)
+            h, step = divmod(r - 5, NC)
+            copies(S_COPIES[r], False)
             gelus(r, 0, NJ)
-            if h >= 0 and step == 0:
-                centre(h)
-            if h >= 0 and step == 1:
-                centred_gain(h)
             if r:
                 regroup(r - 1, 0, NJ)
+                if h >= 0 and step == 2:
+                    rstd(h)
+                copies(V_COPIES[r], True)
+                if r >= 8 and r % NC == 0:
+                    finish(r // NC - 2)
                 quantise_ready_unit()
                 quantise_g(r - 1, 0, NJ)
                 quantise_ready_unit()
-            if h >= 0 and step == 2:
-                finish(h)
+            else:
+                copies(V_COPIES[r], True)
+                quantise_ready_unit()
         gelus(15, 0, 2)
         regroup(14, 0, NJ)
-        finish(2)
+        rstd(2)
         quantise_g(14, 0, NJ)
-        for j0, j1, k0, k1 in ((2, 3, 0, 2), (3, 4, 2, 3)):
-            gelus(15, j0, j1)
-            regroup(15, k0, k1)
-            quantise_g(15, k0, k1)
+        gelus(15, 2, 4)
         table_out = const.tile([P, 1], F32, name="table_out")
         nc.scalar.activation(
             out=table_out[:], in_=gp_t[15][:, 3, T - 1 : T], func=ACT.Abs_reciprocal_sqrt, bias=1.0, scale=0.0
         )
-        regroup(15, 3, 4)
-        quantise_g(15, 3, 4)
-        last_head(0, 2)
-        last_head(2, 3)
-        last_head(3, 4)
+        regroup(15, 0, 2)
+        quantise_g(15, 0, 2)
+        regroup(15, 2, 4)
+        first_half()
+        quantise_g(15, 2, 4)
+        last_matmuls(2, 4)
+        first_half_centre()
+        first_half_gain()
+        finish(2)
+        last_biased(2)
+        last_stats(2)
+        last_gain(2)
+        first_half_finish()
+        last_finish(2)
         assert k["copies"] == 40 and len(w_ops) == 20 and k["fc"] == 64

@@ -217,15 +217,17 @@ def tile_tftdictblock_pa_kernel(
                 if j1 == NJ:
                     first_matmuls_ahead(4 * r + t + 1)
 
-        def regroup(r, j0, j1):
+        def regroup(r, j0, j1, on_scalar=False):
             if j0 == 0:
                 gg = ggp.tile([P, T, 4], BF16, name="gg", tag="gg", align_bytes=64)
                 gg_t[r] = gg
             ns = slice(P * j0, P * j1)
-            nc.vector.tensor_copy(
-                out=gg_t[r][:, ns, :].rearrange("p (n i) t -> p n t i", i=4),
-                in_=gp_t[r][:, :, ns].rearrange("p t (n i) -> p n t i", i=4),
-            )
+            dst = gg_t[r][:, ns, :].rearrange("p (n i) t -> p n t i", i=4)
+            src = gp_t[r][:, :, ns].rearrange("p t (n i) -> p n t i", i=4)
+            if on_scalar:
+                nc.scalar.copy(out=dst, in_=src)
+            else:
+                nc.vector.tensor_copy(out=dst, in_=src)
 
         def quantise_g(r, j0, j1):
             if j0 == 0:
@@ -534,8 +536,8 @@ def tile_tftdictblock_pa_kernel(
             hooks[(r, 1)] = partial(second_matmul, h)
             hooks[(r + 1, 0)] = partial(biased, h)
             hooks[(r + 1, 1)] = partial(centre, h)
-            hooks[(r + 1, 3)] = partial(squared, h)
-            hooks[(r + 2, 0)] = partial(variance, h)
+            hooks[(r + 2, 0)] = partial(squared, h)
+            hooks[(r + 2, 1)] = partial(variance, h)
             if h < H - 2:
                 hooks[(r + 2, 3)] = partial(centred_gain, h)
             else:
@@ -547,12 +549,12 @@ def tile_tftdictblock_pa_kernel(
             gelus(r, 0, NJ)
             if r:
                 regroup(r - 1, 0, NJ)
-                if h >= 0 and step == 2:
-                    rstd(h)
                 copies(V_COPIES[r], True)
                 if r >= 8 and r % NC == 0:
                     finish(r // NC - 2)
                 quantise_ready_unit()
+                if h >= 0 and step == 2:
+                    rstd(h)
                 quantise_g(r - 1, 0, NJ)
                 quantise_ready_unit()
             else:
@@ -560,25 +562,25 @@ def tile_tftdictblock_pa_kernel(
                 quantise_ready_unit()
         gelus(15, 0, 2)
         regroup(14, 0, NJ)
-        rstd(2)
         quantise_g(14, 0, NJ)
+        rstd(2)
         gelus(15, 2, 4)
+        regroup(15, 0, 2)
+        regroup(15, 2, 4, True)
+        quantise_g(15, 0, 2)
+        first_half()
+        quantise_g(15, 2, 4)
+        last_matmuls(2, 4)
+        finish(2)
         table_out = const.tile([P, 1], F32, name="table_out")
         nc.scalar.activation(
             out=table_out[:], in_=gp_t[15][:, 3, T - 1 : T], func=ACT.Abs_reciprocal_sqrt, bias=1.0, scale=0.0
         )
-        regroup(15, 0, 2)
-        quantise_g(15, 0, 2)
-        regroup(15, 2, 4)
-        first_half()
-        quantise_g(15, 2, 4)
-        last_matmuls(2, 4)
         first_half_centre()
-        first_half_gain()
-        finish(2)
         last_biased(2)
         last_stats(2)
         last_gain(2)
-        first_half_finish()
+        first_half_gain()
         last_finish(2)
+        first_half_finish()
         assert k["copies"] == 40 and len(w_ops) == 20 and k["fc"] == 64

@@ -24,12 +24,13 @@ NC = FF // 512
 FLOPS = 2 * T * D * FF * H + 2 * T * FF * HD * H
 
 NTR = 3
+TURN_AT = 0
 NFC = 4
 NPJ = 1
 PJ_POS = {6: 0, 11: 1, 16: 2, 19: 3}
 BC_AFTER = 13
-S_COPIES = [2, 1, 2, 1, 2, 1, 1, 1, 2, 1, 1, 1, 2, 0, 0]
-V_COPIES = [1, 1, 1, 1, 1, 1, 2, 1, 1, 1, 2, 1, 1, 0, 0]
+S_COPIES = [2, 1, 2, 1, 2, 1, 2, 1, 2, 1, 2, 1, 2, 0, 0]
+V_COPIES = [1, 1, 1, 1, 1, 1, 1, 1, 1, 1, 1, 1, 1, 0, 0]
 
 
 def tile_tftdictblock_pa_kernel(
@@ -209,6 +210,8 @@ def tile_tftdictblock_pa_kernel(
             for t in range(4):
                 if j0 == 0:
                     hooks.get((r, t), lambda: None)()
+                    if t == TURN_AT:
+                        transposes_ahead(NTR)
                 first_matmuls_ahead(4 * r + t)
                 nc.scalar.activation(
                     out=gp_t[r][:, t, ns], in_=a_t[(r, t)][:, ns], func=ACT.Gelu,
@@ -545,11 +548,13 @@ def tile_tftdictblock_pa_kernel(
 
         for r in range(15):
             h, step = divmod(r - 5, NC)
-            copies(S_COPIES[r], False)
+            for i in range(S_COPIES[r]):
+                copy_block(False)
             gelus(r, 0, NJ)
             if r:
                 regroup(r - 1, 0, NJ)
-                copies(V_COPIES[r], True)
+                for i in range(V_COPIES[r]):
+                    copy_block(True)
                 if r >= 8 and r % NC == 0:
                     finish(r // NC - 2)
                 quantise_ready_unit()
@@ -558,29 +563,30 @@ def tile_tftdictblock_pa_kernel(
                 quantise_g(r - 1, 0, NJ)
                 quantise_ready_unit()
             else:
-                copies(V_COPIES[r], True)
+                for i in range(V_COPIES[r]):
+                    copy_block(True)
                 quantise_ready_unit()
         gelus(15, 0, 2)
         regroup(14, 0, NJ)
         quantise_g(14, 0, NJ)
         rstd(2)
         gelus(15, 2, 4)
-        regroup(15, 0, 2)
-        regroup(15, 2, 4, True)
-        quantise_g(15, 0, 2)
-        first_half()
-        quantise_g(15, 2, 4)
-        last_matmuls(2, 4)
-        finish(2)
         table_out = const.tile([P, 1], F32, name="table_out")
         nc.scalar.activation(
             out=table_out[:], in_=gp_t[15][:, 3, T - 1 : T], func=ACT.Abs_reciprocal_sqrt, bias=1.0, scale=0.0
         )
+        regroup(15, 0, 2)
+        quantise_g(15, 0, 2)
+        regroup(15, 2, 4)
+        first_half()
+        quantise_g(15, 2, 4)
+        last_matmuls(2, 4)
         first_half_centre()
+        first_half_gain()
+        finish(2)
         last_biased(2)
         last_stats(2)
         last_gain(2)
-        first_half_gain()
-        last_finish(2)
         first_half_finish()
+        last_finish(2)
         assert k["copies"] == 40 and len(w_ops) == 20 and k["fc"] == 64

@@ -29,7 +29,7 @@ NFC = 4
 NPJ = 1
 PJ_POS = {6: 0, 11: 1, 16: 2, 19: 3}
 BC_AFTER = 13
-S_COPIES = [2, 1, 2, 1, 2, 1, 2, 1, 2, 1, 2, 1, 2, 0, 0]
+S_COPIES = [2, 1, 2, 1, 2, 1, 2, 1, 2, 1, 2, 1, 1, 0, 0]
 V_COPIES = [1, 1, 1, 1, 1, 1, 1, 1, 1, 1, 1, 1, 1, 0, 0]
 
 
@@ -443,18 +443,19 @@ def tile_tftdictblock_pa_kernel(
                 out=s[:], in0=xt_sb[:, j, :], scalar=1.0, in1=xe_sb[:, j, :], op0=ALU.mult, op1=ALU.add,
                 accum_out=xsum[:, j : j + 1],
             )
-            nc.vector.tensor_scalar(
-                out=xnm[:, j : j + 1], in0=xsum[:, j : j + 1], scalar1=-1.0 / D, scalar2=None, op0=ALU.mult
-            )
             sq = xpool.tile([P, D], F32, name="xsq", tag="xsq", bufs=2)
             nc.scalar.activation(
-                out=sq[:], in_=s[:], func=ACT.Square, bias=xnm[:, j : j + 1], scale=1.0, accum_out=xss[:, j : j + 1]
+                out=sq[:], in_=s[:], func=ACT.Square, bias=xsum[:, j : j + 1], scale=-1.0 * D,
+                accum_out=xss[:, j : j + 1],
             )
             norm.append(s)
 
         def x_rstd(js):
             nc.vector.tensor_scalar(
-                out=xve[:, js], in0=xss[:, js], scalar1=1.0 / D, scalar2=EPS, op0=ALU.mult, op1=ALU.add
+                out=xve[:, js], in0=xss[:, js], scalar1=1.0 / D**3, scalar2=EPS, op0=ALU.mult, op1=ALU.add
+            )
+            nc.vector.tensor_scalar(
+                out=xnm[:, js], in0=xsum[:, js], scalar1=-1.0 / D, scalar2=None, op0=ALU.mult
             )
             nc.gpsimd.tensor_tensor(out=xrs[:, js], in0=xve[:, js], in1=neg_half4[:, js], op=ALU.pow)
 
@@ -492,6 +493,10 @@ def tile_tftdictblock_pa_kernel(
                     transposes_ahead(NTR)
 
         ctx.enter_context(tc.manual_schedule())
+        warm_ps = ps_fc.tile([P, T], F32, name="warm_ps", tag="fc")
+        for j in range(NJ):
+            nc.tensor.matmul(warm_ps[:], ident_bf[:], xt_sb[:, j, :], start=True, stop=True)
+            nc.tensor.matmul(warm_ps[:], ident_bf[:], xe_sb[:, j, :], start=True, stop=True)
         transposes_ahead(2)
         x_add(0)
         x_add(1)
@@ -502,12 +507,13 @@ def tile_tftdictblock_pa_kernel(
             u, e = divmod(t, 2)
             nc.tensor.transpose(cols_ps[:, t, :], vec_a[:, 256 * u + e : 256 * (u + 1) : 2], ident_bf[:])
         nc.tensor.transpose(cols_ps[:, 4, :], vec_a[:, 0:P], ident_bf[:])
-        transposes_ahead(NTR)
+        transposes_ahead(3)
         x_norm(0)
         x_norm(1)
         x_rstd(slice(2, 4))
         nc.vector.tensor_copy(out=cols[:], in_=cols_ps[:, :, 0:28])
         copies(1, False)
+        copies(1, True)
         x_norm(2)
         x_norm(3)
         copies(2, False)
@@ -566,11 +572,21 @@ def tile_tftdictblock_pa_kernel(
                 for i in range(V_COPIES[r]):
                     copy_block(True)
                 quantise_ready_unit()
+        warm_tail = ps_tr.tile([P, 2 * P], F32, name="warm_tail", tag="tr")
+
+        def keep_warm(j0, j1):
+            for t in range(4):
+                nc.tensor.matmul(
+                    warm_tail[:], ident_bf[:], gp_t[15][:, t, P * j0 : P * j1], start=True, stop=True
+                )
+
         gelus(15, 0, 2)
+        keep_warm(0, 2)
         regroup(14, 0, NJ)
         quantise_g(14, 0, NJ)
         rstd(2)
         gelus(15, 2, 4)
+        keep_warm(2, 4)
         table_out = const.tile([P, 1], F32, name="table_out")
         nc.scalar.activation(
             out=table_out[:], in_=gp_t[15][:, 3, T - 1 : T], func=ACT.Abs_reciprocal_sqrt, bias=1.0, scale=0.0

@@ -29,8 +29,8 @@ NFC = 4
 NPJ = 1
 PJ_POS = {6: 0, 11: 1, 16: 2, 19: 3}
 BC_AFTER = 13
-S_COPIES = [2, 1, 2, 1, 2, 1, 2, 1, 2, 1, 2, 1, 1, 0, 0]
-V_COPIES = [1, 1, 1, 1, 1, 1, 1, 1, 1, 1, 1, 1, 1, 0, 0]
+S_COPIES = [2, 1, 2, 1, 2, 2, 2, 2, 2, 2, 2, 1, 1, 0, 0]
+V_COPIES = [1, 1, 1, 1, 1, 1, 1, 0, 1, 0, 1, 0, 1, 0, 0]
 
 
 def tile_tftdictblock_pa_kernel(
@@ -42,7 +42,7 @@ def tile_tftdictblock_pa_kernel(
         xpool = ctx.enter_context(tc.tile_pool(name="xpool", bufs=1))
         small = ctx.enter_context(tc.tile_pool(name="small", bufs=4))
         rawp = ctx.enter_context(tc.tile_pool(name="rawp", bufs=12))
-        wgp = ctx.enter_context(tc.tile_pool(name="wgp", bufs=9))
+        wgp = ctx.enter_context(tc.tile_pool(name="wgp", bufs=8))
         wcp = ctx.enter_context(tc.tile_pool(name="wcp", bufs=12))
         pcp = ctx.enter_context(tc.tile_pool(name="pcp", bufs=4))
         gpp = ctx.enter_context(tc.tile_pool(name="gpp", bufs=3))
@@ -201,6 +201,7 @@ def tile_tftdictblock_pa_kernel(
                 k["fc"] += 1
 
         hooks = {}
+        turn_back_at = {}
 
         def gelus(r, j0, j1):
             if j0 == 0:
@@ -212,6 +213,8 @@ def tile_tftdictblock_pa_kernel(
                     hooks.get((r, t), lambda: None)()
                     if t == TURN_AT:
                         transposes_ahead(NTR)
+                        if r in turn_back_at:
+                            turned_back(turn_back_at[r])
                 first_matmuls_ahead(4 * r + t)
                 nc.scalar.activation(
                     out=gp_t[r][:, t, ns], in_=a_t[(r, t)][:, ns], func=ACT.Gelu,
@@ -303,6 +306,35 @@ def tile_tftdictblock_pa_kernel(
                     cw_ps[:, j, :], ln_t[h]["pt"][:, P * j : P * (j + 1)], cdw[:, h, :], start=True, stop=True
                 )
             ln_t[h]["cw"] = cw_ps
+
+        def turned_back(h):
+            pb_ps = ps_pj.tile([P, NJ, HD], F32, name="pb_ps", tag="pj")
+            for j in range(NJ):
+                nc.tensor.transpose(pb_ps[:, j, :], ln_t[h]["pt"][:, P * j : P * (j + 1)], ident_f[:])
+            ln_t[h]["pb"] = pb_ps
+
+        def stats(h):
+            st4 = small.tile([P, NJ, 6], F32, name="st4", tag="st4")
+            mv4 = small.tile([P, NJ, 2], F32, name="mv4", tag="mv4")
+            for j in range(NJ):
+                nc.vector.bn_stats(out=st4[:, j, :], in_=ln_t[h]["pb"][:, j, :])
+            for j in range(NJ):
+                nc.vector.bn_aggr(out=mv4[:, j, :], in_=st4[:, j, :])
+            ve = small.tile([P, NJ], F32, name="ve", tag="ve")
+            nc.vector.tensor_scalar(out=ve[:], in0=mv4[:, :, 1], scalar1=EPS, scalar2=None, op0=ALU.add)
+            rs = small.tile([P, NJ], F32, name="rs", tag="rs")
+            nc.gpsimd.tensor_tensor(out=rs[:], in0=ve[:], in1=neg_half4[:], op=ALU.pow)
+            ln_t[h]["mv"] = mv4
+            ln_t[h]["rs"] = rs
+
+        def gain(h):
+            t1 = fin.tile([P, NJ, HD], F32, name="t1h", tag="t1h")
+            for j in range(NJ):
+                nc.vector.scalar_tensor_tensor(
+                    out=t1[:, j, :], in0=ln_t[h]["pb"][:, j, :], scalar=ln_t[h]["mv"][:, j, 0:1],
+                    in1=dw_bc[:, HD * h : HD * (h + 1)], op0=ALU.subtract, op1=ALU.mult,
+                )
+            ln_t[h]["cw"] = t1
 
         def finish(h):
             s = ln_t[h]
@@ -544,12 +576,12 @@ def tile_tftdictblock_pa_kernel(
             r = NC * h + 5
             hooks[(r, 1)] = partial(second_matmul, h)
             hooks[(r + 1, 0)] = partial(biased, h)
-            hooks[(r + 1, 1)] = partial(centre, h)
-            hooks[(r + 2, 0)] = partial(squared, h)
-            hooks[(r + 2, 1)] = partial(variance, h)
             if h < H - 2:
-                hooks[(r + 2, 3)] = partial(centred_gain, h)
+                turn_back_at[r + 2] = h
             else:
+                hooks[(r + 1, 1)] = partial(centre, h)
+                hooks[(r + 2, 0)] = partial(squared, h)
+                hooks[(r + 2, 1)] = partial(variance, h)
                 hooks[(r + 1, 2)] = partial(centred_gain, h)
 
         for r in range(15):
@@ -559,14 +591,18 @@ def tile_tftdictblock_pa_kernel(
             gelus(r, 0, NJ)
             if r:
                 regroup(r - 1, 0, NJ)
+                ready = k["copies"] // 2
                 for i in range(V_COPIES[r]):
                     copy_block(True)
                 if r >= 8 and r % NC == 0:
                     finish(r // NC - 2)
-                quantise_ready_unit()
                 if h >= 0 and step == 2:
-                    rstd(h)
+                    stats(h)
+                if len(w_ops) < ready:
+                    quantise_ready_unit()
                 quantise_g(r - 1, 0, NJ)
+                if h >= 0 and step == 2:
+                    gain(h)
                 quantise_ready_unit()
             else:
                 for i in range(V_COPIES[r]):
@@ -584,7 +620,6 @@ def tile_tftdictblock_pa_kernel(
         keep_warm(0, 2)
         regroup(14, 0, NJ)
         quantise_g(14, 0, NJ)
-        rstd(2)
         gelus(15, 2, 4)
         keep_warm(2, 4)
         table_out = const.tile([P, 1], F32, name="table_out")
@@ -592,6 +627,7 @@ def tile_tftdictblock_pa_kernel(
             out=table_out[:], in_=gp_t[15][:, 3, T - 1 : T], func=ACT.Abs_reciprocal_sqrt, bias=1.0, scale=0.0
         )
         regroup(15, 0, 2)
+        rstd(2)
         quantise_g(15, 0, 2)
         regroup(15, 2, 4)
         first_half()

@@ -19,18 +19,23 @@ H = 4
 FF = 2048
 HD = 128
 EPS = 1e-5
-NJ = T // P
-NC = FF // 512
 FLOPS = 2 * T * D * FF * H + 2 * T * FF * HD * H
 
-NTR = 3
-TURN_AT = 0
-NFC = 4
-NPJ = 1
-PJ_POS = {6: 0, 11: 1, 16: 2, 19: 3}
-BC_AFTER = 13
-S_COPIES = [2, 1, 2, 1, 2, 2, 2, 2, 2, 2, 2, 1, 1, 0, 0]
-V_COPIES = [1, 1, 1, 1, 1, 1, 1, 0, 1, 0, 1, 0, 1, 0, 0]
+TILES = T // P
+GROUPS = FF // 512
+ALL_GROUPS = H * GROUPS
+PACK = 4
+RUN = 4
+HALF = T // 2
+LAST = H - 1
+
+TURN_BANKS = 3
+FIRST_BANKS = 4
+
+PROJ_AT = {6: 0, 11: 1, 16: 2, 19: 3}
+UNITS = 20
+BLOCKS = 2 * UNITS
+NORM_VECTORS_AFTER = 13
 
 
 def tile_tftdictblock_pa_kernel(
@@ -50,595 +55,553 @@ def tile_tftdictblock_pa_kernel(
         gcp = ctx.enter_context(tc.tile_pool(name="gcp", bufs=8))
         fin = ctx.enter_context(tc.tile_pool(name="fin", bufs=2))
         tail = ctx.enter_context(tc.tile_pool(name="tail", bufs=3))
-        ps_tr = ctx.enter_context(tc.psum_pool(name="ps_tr", bufs=NTR))
-        ps_fc = ctx.enter_context(tc.psum_pool(name="ps_fc", bufs=NFC))
-        ps_pj = ctx.enter_context(tc.psum_pool(name="ps_pj", bufs=NPJ))
+        ps_turn = ctx.enter_context(tc.psum_pool(name="ps_turn", bufs=TURN_BANKS))
+        ps_first = ctx.enter_context(tc.psum_pool(name="ps_first", bufs=FIRST_BANKS))
+        ps_second = ctx.enter_context(tc.psum_pool(name="ps_second", bufs=1))
 
-        units = []
-        quad = 0
-        for pos in range(20):
-            if pos in PJ_POS:
-                units.append(("pj", PJ_POS[pos]))
-            else:
-                units.append(("fc", quad))
-                quad += 1
-        unit_of_quad = {}
+        unit_kind = []
+        unit_of_group = []
         unit_of_head = {}
-        for pos, (kind, idx) in enumerate(units):
-            if kind == "fc":
-                unit_of_quad[idx] = pos
+        for pos in range(UNITS):
+            if pos in PROJ_AT:
+                unit_of_head[PROJ_AT[pos]] = pos
+                unit_kind.append(("proj", PROJ_AT[pos]))
             else:
-                unit_of_head[idx] = pos
+                unit_kind.append(("fc", len(unit_of_group)))
+                unit_of_group.append(pos)
 
-        vec_a = const.tile([P, 512], BF16, name="vec_a")
-        nc.gpsimd.memset(vec_a[:], 0.0)
-        nc.scalar.dma_start(out=vec_a[0:1, :], in_=ln2_w.rearrange("(o d) -> o d", o=1))
-        nc.scalar.dma_start(out=vec_a[1:2, :], in_=ln2_b.rearrange("(o d) -> o d", o=1))
-        nc.scalar.dma_start(out=vec_a[8:24, :], in_=fc_b.rearrange("h (c x) -> (h c) x", x=512))
-        nc.scalar.dma_start(out=vec_a[24:28, 0:P], in_=proj_b)
-        warm_in = const.tile([P, 1], F32, name="warm_in")
-        warm_out = const.tile([P, 1], F32, name="warm_out")
-        nc.vector.memset(warm_in[:], 0.0)
-        nc.scalar.activation(out=warm_out[:], in_=warm_in[:], func=ACT.Gelu)
-        neg_half4 = const.tile([P, NJ], F32, name="neg_half4")
-        inv_col = const.tile([P, 1], F32, name="inv_col")
-        nc.vector.memset(inv_col[:], 1.0 / HD)
-        nc.vector.memset(neg_half4[:], -0.5)
-        eps_col = const.tile([P, 1], F32, name="eps_col")
-        nc.vector.tensor_scalar(
-            out=eps_col[:], in0=warm_in[:], scalar1=EPS, scalar2=None, op0=ALU.add
-        )
+        vectors = const.tile([P, 512], BF16, name="vectors")
+        nc.gpsimd.memset(vectors[:], 0.0)
+        nc.scalar.dma_start(out=vectors[0:1, :], in_=ln2_w.rearrange("(o d) -> o d", o=1))
+        nc.scalar.dma_start(out=vectors[1:2, :], in_=ln2_b.rearrange("(o d) -> o d", o=1))
+        nc.scalar.dma_start(out=vectors[8:24, :], in_=fc_b.rearrange("h (c x) -> (h c) x", x=512))
+        nc.scalar.dma_start(out=vectors[24:28, 0:P], in_=proj_b)
+        zero = const.tile([P, 1], F32, name="zero")
+        gelu_of_zero = const.tile([P, 1], F32, name="gelu_of_zero")
+        nc.vector.memset(zero[:], 0.0)
+        nc.scalar.activation(out=gelu_of_zero[:], in_=zero[:], func=ACT.Gelu)
+        minus_half = const.tile([P, TILES], F32, name="minus_half")
+        mean_weight = const.tile([P, 1], F32, name="mean_weight")
+        nc.vector.memset(mean_weight[:], 1.0 / HD)
+        nc.vector.memset(minus_half[:], -0.5)
+        eps = const.tile([P, 1], F32, name="eps")
+        nc.vector.tensor_scalar(out=eps[:], in0=zero[:], scalar1=EPS, scalar2=None, op0=ALU.add)
         ident_bf = const.tile([P, P], BF16, name="ident_bf")
         ident_f = const.tile([P, P], F32, name="ident_f")
         make_identity(nc, ident_bf[:])
         make_identity(nc, ident_f[:])
 
-        xt_v = xt_new.rearrange("b (p j) d -> p (b j) d", j=NJ)
-        xe_v = xe.rearrange("b (p j) d -> p (b j) d", j=NJ)
-        xt_sb = xpool.tile([P, NJ, D], BF16, name="xt_sb")
-        xe_sb = xpool.tile([P, NJ, D], BF16, name="xe_sb")
-        raws = []
-        tail_bc = []
+        xt_view = xt_new.rearrange("b (p j) d -> p (b j) d", j=TILES)
+        xe_view = xe.rearrange("b (p j) d -> p (b j) d", j=TILES)
+        xt_sb = xpool.tile([P, TILES, D], BF16, name="xt_sb")
+        xe_sb = xpool.tile([P, TILES, D], BF16, name="xe_sb")
+        for js in (slice(0, 1), slice(1, 2), slice(2, 4)):
+            nc.sync.dma_start(out=xt_sb[:, js, :], in_=xt_view[:, js, :])
+            nc.sync.dma_start(out=xe_sb[:, js, :], in_=xe_view[:, js, :])
 
-        def load_x(j0, j1):
-            js = slice(j0, j1)
-            nc.sync.dma_start(out=xt_sb[:, js, :], in_=xt_v[:, js, :])
-            nc.sync.dma_start(out=xe_sb[:, js, :], in_=xe_v[:, js, :])
-
-        def load_unit(pos):
-            kind, idx = units[pos]
+        raw_of_unit = []
+        norm_vectors = []
+        for pos in range(UNITS):
+            kind, index = unit_kind[pos]
             raw = rawp.tile([P, 2048], BF16, name="raw", tag="raw")
             if kind == "fc":
-                h, c = divmod(idx, NC)
+                h, c = divmod(index, GROUPS)
                 nc.sync.dma_start(
                     out=raw[:].rearrange("p (u x) -> p u x", u=2),
                     in_=fc_w[h, 512 * c : 512 * (c + 1), :].rearrange("(u p e) k -> p u (e k)", u=2, e=2),
                 )
             else:
-                nc.sync.dma_start(out=raw[:], in_=proj_w[idx, :, :])
-            raws.append(raw)
+                nc.sync.dma_start(out=raw[:], in_=proj_w[index, :, :])
+            raw_of_unit.append(raw)
+            if pos == NORM_VECTORS_AFTER:
+                for name, vec in (("gain_rows", dln_w), ("bias_rows", dln_b)):
+                    rows = const.tile([P, H * HD], BF16, name=name)
+                    nc.sync.dma_start(out=rows[:], in_=vec.rearrange("h d -> (h d)").partition_broadcast(P))
+                    norm_vectors.append(rows)
+        gain_rows, bias_rows = norm_vectors
+        last_proj_bias = const.tile([P, HD], BF16, name="last_proj_bias")
+        nc.sync.dma_start(out=last_proj_bias[:], in_=proj_b[LAST, :].partition_broadcast(P))
 
-        load_x(0, 1)
-        load_x(1, 2)
-        load_x(2, 4)
-        load_unit(0)
-        for pos in range(1, 20):
-            load_unit(pos)
-            if pos == BC_AFTER:
-                for r, vec in enumerate((dln_w, dln_b)):
-                    bc = const.tile([P, 512], BF16, name="bc%d" % r)
-                    nc.sync.dma_start(out=bc[:], in_=vec.rearrange("h d -> (h d)").partition_broadcast(P))
-                    tail_bc.append(bc)
-        dw_bc, db_bc = tail_bc
-        pb_bc = const.tile([P, HD], BF16, name="pb_bc")
-        nc.sync.dma_start(out=pb_bc[:], in_=proj_b[H - 1, :].partition_broadcast(P))
+        columns_ps = ps_second.tile([P, 5, P], BF16, name="columns_ps", tag="second")
+        columns = const.tile([P, 5, 28], F32, name="columns")
 
-        cols_ps = ps_pj.tile([P, 5, P], BF16, name="cols_ps", tag="pj")
-        cols = const.tile([P, 5, 28], F32, name="cols")
+        x2_planar = xpool.tile([P, PACK, T], BF16, name="x2_planar")
+        x2_words = xpool.tile([P, T, PACK], BF16, name="x2_words", align_bytes=64)
+        x2_codes = xpool.tile([P, T], U32, name="x2_codes", align_bytes=64)
+        x2_scales = xpool.tile([P, T], U8, name="x2_scales", align_bytes=64)
 
-        x2p = xpool.tile([P, 4, T], BF16, name="x2p")
-        x2g = xpool.tile([P, T, 4], BF16, name="x2g", align_bytes=64)
-        xc = xpool.tile([P, T], U32, name="xc", align_bytes=64)
-        xs = xpool.tile([P, T], U8, name="xs", align_bytes=64)
+        turned = []
+        weight_words = []
+        weight_ops = []
+        count = {"copied": 0, "first": 0}
 
-        tr_t = []
-        wg_t = []
-        w_ops = []
-        k = {"copies": 0, "fc": 0}
-
-        def transpose_block():
-            u, b = divmod(len(tr_t), 2)
-            raw32 = raws[u][:].bitcast(F32)
-            tr = ps_tr.tile([P, 512], F32, name="tr", tag="tr")
-            for q in range(4):
-                blk = 4 * b + q
-                nc.tensor.transpose(tr[:, P * q : P * (q + 1)], raw32[:, P * blk : P * (blk + 1)], ident_f[:])
-            tr_t.append(tr)
-
-        def transposes_ahead(n):
-            while len(tr_t) < min(k["copies"] + n, 40):
-                transpose_block()
+        def turn_blocks(ahead):
+            while len(turned) < min(count["copied"] + ahead, BLOCKS):
+                unit, b = divmod(len(turned), 2)
+                words = raw_of_unit[unit][:].bitcast(F32)
+                bank = ps_turn.tile([P, 512], F32, name="bank", tag="turn")
+                for q in range(4):
+                    first = 512 * b + P * q
+                    nc.tensor.transpose(bank[:, P * q : P * (q + 1)], words[:, first : first + P], ident_f[:])
+                turned.append(bank)
 
         def copy_block(on_vector):
-            u, b = divmod(k["copies"], 2)
+            unit, b = divmod(count["copied"], 2)
             if b == 0:
-                wg = wgp.tile([P, 2048], BF16, name="wg", tag="wg", align_bytes=64)
-                wg_t.append(wg)
-            dst = wg_t[u][:].bitcast(F32)[:, 512 * b : 512 * (b + 1)].rearrange("p (i f u) -> p i f u", i=2, u=2)
-            src = tr_t[k["copies"]][:].rearrange("p (i u f) -> p i f u", i=2, u=2)
+                words = wgp.tile([P, 2048], BF16, name="words", tag="words", align_bytes=64)
+                weight_words.append(words)
+            dst = weight_words[unit][:].bitcast(F32)[:, 512 * b : 512 * (b + 1)]
+            dst = dst.rearrange("p (i f u) -> p i f u", i=2, u=2)
+            src = turned[count["copied"]][:].rearrange("p (i u f) -> p i f u", i=2, u=2)
             if on_vector:
                 nc.vector.tensor_copy(out=dst, in_=src)
             else:
                 nc.scalar.copy(out=dst, in_=src)
-            k["copies"] += 1
+            count["copied"] += 1
 
-        def quantise_ready_unit():
-            u = len(w_ops)
-            if 2 * (u + 1) > k["copies"]:
+        def copy_and_turn(on_vector):
+            copy_block(on_vector)
+            turn_blocks(TURN_BANKS)
+
+        def quantise_unit_if_copied():
+            unit = len(weight_ops)
+            if 2 * unit + 2 > count["copied"]:
                 return
-            pool = wcp if units[u][0] == "fc" else pcp
+            pool = wcp if unit_kind[unit][0] == "fc" else pcp
             codes = pool.tile([P, 512], U32, name="codes", tag="codes", align_bytes=64)
             scales = pool.tile([P, 512], U8, name="scales", tag="scales", align_bytes=64)
-            nc.vector.quantize_mx(out=codes[:].bitcast(FP8X4), scales=scales[:], in_=wg_t[u][:])
-            w_ops.append((codes, scales))
+            nc.vector.quantize_mx(out=codes[:].bitcast(FP8X4), scales=scales[:], in_=weight_words[unit][:])
+            weight_ops.append((codes, scales))
 
-        a_t = {}
-        gp_t = {}
-        gg_t = {}
-        g_ops = {}
+        first_ps = {}
+        gelu_planar = {}
+        gelu_words = {}
+        gelu_ops = {}
 
-        def first_matmuls_ahead(done):
-            while k["fc"] < min(done + NFC, 64) and unit_of_quad[k["fc"] // 4] < len(w_ops):
-                r, t = divmod(k["fc"], 4)
-                wc, ws = w_ops[unit_of_quad[r]]
-                a_ps = ps_fc.tile([P, T], F32, name="a_ps", tag="fc")
-                cs = slice(P * t, P * (t + 1))
+        def first_passes(emptied):
+            while count["first"] < min(emptied + FIRST_BANKS, PACK * ALL_GROUPS):
+                r, t = divmod(count["first"], PACK)
+                if unit_of_group[r] >= len(weight_ops):
+                    return
+                codes, scales = weight_ops[unit_of_group[r]]
+                product = ps_first.tile([P, T], F32, name="product", tag="first")
+                cols = slice(P * t, P * (t + 1))
                 nc.tensor.matmul_mx(
-                    out=a_ps[:], lhsT=wc[:, cs].bitcast(FP8X4), lhsT_scale=ws[:, cs],
-                    rhs=xc[:].bitcast(FP8X4), rhs_scale=xs[:], start=True, stop=True,
+                    out=product[:], lhsT=codes[:, cols].bitcast(FP8X4), lhsT_scale=scales[:, cols],
+                    rhs=x2_codes[:].bitcast(FP8X4), rhs_scale=x2_scales[:], start=True, stop=True,
                 )
-                a_t[(r, t)] = a_ps
-                k["fc"] += 1
+                first_ps[(r, t)] = product
+                count["first"] += 1
 
-        hooks = {}
-        turn_back_at = {}
+        before_gelu = {}
+
+        def at(r, t, step):
+            before_gelu.setdefault((r, t), []).append(step)
 
         def gelus(r, j0, j1):
             if j0 == 0:
-                gp = gpp.tile([P, 4, T], BF16, name="gp", tag="gp")
-                gp_t[r] = gp
-            ns = slice(P * j0, P * j1)
-            for t in range(4):
+                planar = gpp.tile([P, PACK, T], BF16, name="planar", tag="planar")
+                gelu_planar[r] = planar
+            tokens = slice(P * j0, P * j1)
+            for t in range(PACK):
                 if j0 == 0:
-                    hooks.get((r, t), lambda: None)()
-                    if t == TURN_AT:
-                        transposes_ahead(NTR)
-                        if r in turn_back_at:
-                            turned_back(turn_back_at[r])
-                first_matmuls_ahead(4 * r + t)
+                    for step in before_gelu.get((r, t), []):
+                        step()
+                first_passes(PACK * r + t)
                 nc.scalar.activation(
-                    out=gp_t[r][:, t, ns], in_=a_t[(r, t)][:, ns], func=ACT.Gelu,
-                    bias=cols[:, t, 8 + r : 9 + r], scale=1.0,
+                    out=gelu_planar[r][:, t, tokens], in_=first_ps[(r, t)][:, tokens], func=ACT.Gelu,
+                    bias=columns[:, t, 8 + r : 9 + r], scale=1.0,
                 )
-                if j1 == NJ:
-                    first_matmuls_ahead(4 * r + t + 1)
+                if j1 == TILES:
+                    first_passes(PACK * r + t + 1)
 
-        def regroup(r, j0, j1, on_scalar=False):
-            if j0 == 0:
-                gg = ggp.tile([P, T, 4], BF16, name="gg", tag="gg", align_bytes=64)
-                gg_t[r] = gg
-            ns = slice(P * j0, P * j1)
-            dst = gg_t[r][:, ns, :].rearrange("p (n i) t -> p n t i", i=4)
-            src = gp_t[r][:, :, ns].rearrange("p t (n i) -> p n t i", i=4)
-            if on_scalar:
-                nc.scalar.copy(out=dst, in_=src)
-            else:
-                nc.vector.tensor_copy(out=dst, in_=src)
-
-        def quantise_g(r, j0, j1):
-            if j0 == 0:
-                gc = gcp.tile([P, T], U32, name="gc", tag="gc", align_bytes=64)
-                gs = gcp.tile([P, T], U8, name="gs", tag="gs", align_bytes=64)
-                g_ops[r] = (gc, gs)
-            gc, gs = g_ops[r]
-            ns = slice(P * j0, P * j1)
-            nc.vector.quantize_mx(
-                out=gc[:, ns].bitcast(FP8X4), scales=gs[:, ns],
-                in_=gg_t[r][:, ns, :].rearrange("p n t -> p (n t)"),
+        def regroup(dst, src):
+            nc.vector.tensor_copy(
+                out=dst.rearrange("p (n i) t -> p n t i", i=RUN), in_=src.rearrange("p t (n i) -> p n t i", i=RUN)
             )
 
-        ln_t = {}
-        cmat = const.tile([P, HD], F32, name="cmat")
-        cdw = const.tile([P, H, HD], F32, name="cdw")
+        def regroup_gelus(r, j0, j1):
+            if j0 == 0:
+                words = ggp.tile([P, T, PACK], BF16, name="words_g", tag="words_g", align_bytes=64)
+                gelu_words[r] = words
+            tokens = slice(P * j0, P * j1)
+            regroup(gelu_words[r][:, tokens, :], gelu_planar[r][:, :, tokens])
 
-        def second_matmul(h):
-            pc, pscale = w_ops[unit_of_head[h]]
-            pt_ps = ps_pj.tile([P, T], F32, name="pt_ps", tag="pj")
-            for c in range(NC):
-                gc, gs = g_ops[NC * h + c]
+        def quantise_gelus(r, j0, j1):
+            if j0 == 0:
+                codes = gcp.tile([P, T], U32, name="codes_g", tag="codes_g", align_bytes=64)
+                scales = gcp.tile([P, T], U8, name="scales_g", tag="scales_g", align_bytes=64)
+                gelu_ops[r] = (codes, scales)
+            codes, scales = gelu_ops[r]
+            tokens = slice(P * j0, P * j1)
+            nc.vector.quantize_mx(
+                out=codes[:, tokens].bitcast(FP8X4), scales=scales[:, tokens],
+                in_=gelu_words[r][:, tokens, :].rearrange("p n t -> p (n t)"),
+            )
+
+        head = {}
+        centring = const.tile([P, HD], F32, name="centring")
+        centring_gain = const.tile([P, H, HD], F32, name="centring_gain")
+
+        def second_passes(bank, h, tokens):
+            codes_w, scales_w = weight_ops[unit_of_head[h]]
+            for c in range(GROUPS):
+                codes, scales = gelu_ops[GROUPS * h + c]
+                cols = slice(P * c, P * (c + 1))
                 nc.tensor.matmul_mx(
-                    out=pt_ps[:],
-                    lhsT=pc[:, P * c : P * (c + 1)].bitcast(FP8X4), lhsT_scale=pscale[:, P * c : P * (c + 1)],
-                    rhs=gc[:].bitcast(FP8X4), rhs_scale=gs[:],
-                    start=(c == 0), stop=(c == NC - 1),
+                    out=bank[:], lhsT=codes_w[:, cols].bitcast(FP8X4), lhsT_scale=scales_w[:, cols],
+                    rhs=codes[:, tokens].bitcast(FP8X4), rhs_scale=scales[:, tokens],
+                    start=(c == 0), stop=(c == GROUPS - 1),
                 )
-            ln_t[h] = {"pt_ps": pt_ps}
+
+        def add_proj_bias(out_tile, bank, h):
+            nc.scalar.activation(
+                out=out_tile[:], in_=bank[:], func=ACT.Identity, bias=columns[:, 4, 24 + h : 25 + h], scale=1.0
+            )
+
+        def second_product(h):
+            bank = ps_second.tile([P, T], F32, name="product2", tag="second")
+            second_passes(bank, h, slice(0, T))
+            head[h] = {"product": bank}
 
         def biased(h):
-            pt = fin.tile([P, T], F32, name="pt", tag="pt")
-            nc.scalar.activation(
-                out=pt[:], in_=ln_t[h]["pt_ps"][:], func=ACT.Identity, bias=cols[:, 4, 24 + h : 25 + h], scale=1.0
-            )
-            ln_t[h]["pt"] = pt
+            on_channels = fin.tile([P, T], F32, name="on_channels", tag="on_channels")
+            add_proj_bias(on_channels, head[h]["product"], h)
+            head[h]["on_channels"] = on_channels
 
-        def centre(h):
-            ct_ps = ps_pj.tile([P, T], F32, name="ct_ps", tag="pj")
-            nc.tensor.matmul(ct_ps[:], cmat[:], ln_t[h]["pt"][:], start=True, stop=True)
-            ln_t[h]["ct"] = ct_ps
+        def centred(h):
+            bank = ps_second.tile([P, T], F32, name="centred", tag="second")
+            nc.tensor.matmul(bank[:], centring[:], head[h]["on_channels"][:], start=True, stop=True)
+            head[h]["centred"] = bank
 
         def squared(h):
-            sq = fin.tile([P, T], F32, name="sq", tag="sq")
-            nc.scalar.activation(out=sq[:], in_=ln_t[h]["ct"][:], func=ACT.Square)
-            ln_t[h]["sq"] = sq
+            squares = fin.tile([P, T], F32, name="squares", tag="squares")
+            nc.scalar.activation(out=squares[:], in_=head[h]["centred"][:], func=ACT.Square)
+            head[h]["squares"] = squares
+
+        def average_squares(bank, squares, tiles):
+            for j in range(tiles):
+                nc.tensor.matmul(
+                    bank[:, j : j + 1], squares[:, P * j : P * (j + 1)], mean_weight[:], start=True, stop=True
+                )
+
+        def gained(bank, on_channels, h, tiles):
+            for j in range(tiles):
+                nc.tensor.matmul(
+                    bank[:, j, :], on_channels[:, P * j : P * (j + 1)], centring_gain[:, h, :], start=True, stop=True
+                )
 
         def variance(h):
-            vs_ps = ps_pj.tile([P, NJ], F32, name="vs_ps", tag="pj")
-            for j in range(NJ):
-                nc.tensor.matmul(
-                    vs_ps[:, j : j + 1], ln_t[h]["sq"][:, P * j : P * (j + 1)], inv_col[:], start=True, stop=True
-                )
-            ln_t[h]["vs"] = vs_ps
-
-        def rstd(h):
-            ve = small.tile([P, NJ], F32, name="ve", tag="ve")
-            nc.vector.tensor_scalar(out=ve[:], in0=ln_t[h]["vs"][:], scalar1=EPS, scalar2=None, op0=ALU.add)
-            rs = small.tile([P, NJ], F32, name="rs", tag="rs")
-            nc.gpsimd.tensor_tensor(out=rs[:], in0=ve[:], in1=neg_half4[:], op=ALU.pow)
-            ln_t[h]["rs"] = rs
+            bank = ps_second.tile([P, TILES], F32, name="variance", tag="second")
+            average_squares(bank, head[h]["squares"], TILES)
+            head[h]["variance"] = bank[:]
 
         def centred_gain(h):
-            if h == H - 2:
-                cw_ps = ps_tr.tile([P, NJ, HD], F32, name="cw_ps2", tag="tr")
-            else:
-                cw_ps = ps_pj.tile([P, NJ, HD], F32, name="cw_ps", tag="pj")
-            for j in range(NJ):
-                nc.tensor.matmul(
-                    cw_ps[:, j, :], ln_t[h]["pt"][:, P * j : P * (j + 1)], cdw[:, h, :], start=True, stop=True
-                )
-            ln_t[h]["cw"] = cw_ps
+            bank = ps_turn.tile([P, TILES, HD], F32, name="centred_gain", tag="turn")
+            gained(bank, head[h]["on_channels"], h, TILES)
+            head[h]["gained"] = bank
 
         def turned_back(h):
-            pb_ps = ps_pj.tile([P, NJ, HD], F32, name="pb_ps", tag="pj")
-            for j in range(NJ):
-                nc.tensor.transpose(pb_ps[:, j, :], ln_t[h]["pt"][:, P * j : P * (j + 1)], ident_f[:])
-            ln_t[h]["pb"] = pb_ps
+            bank = ps_second.tile([P, TILES, HD], F32, name="on_tokens", tag="second")
+            for j in range(TILES):
+                nc.tensor.transpose(bank[:, j, :], head[h]["on_channels"][:, P * j : P * (j + 1)], ident_f[:])
+            head[h]["on_tokens"] = bank
 
-        def stats(h):
-            st4 = small.tile([P, NJ, 6], F32, name="st4", tag="st4")
-            mv4 = small.tile([P, NJ, 2], F32, name="mv4", tag="mv4")
-            for j in range(NJ):
-                nc.vector.bn_stats(out=st4[:, j, :], in_=ln_t[h]["pb"][:, j, :])
-            for j in range(NJ):
-                nc.vector.bn_aggr(out=mv4[:, j, :], in_=st4[:, j, :])
-            ve = small.tile([P, NJ], F32, name="ve", tag="ve")
-            nc.vector.tensor_scalar(out=ve[:], in0=mv4[:, :, 1], scalar1=EPS, scalar2=None, op0=ALU.add)
-            rs = small.tile([P, NJ], F32, name="rs", tag="rs")
-            nc.gpsimd.tensor_tensor(out=rs[:], in0=ve[:], in1=neg_half4[:], op=ALU.pow)
-            ln_t[h]["mv"] = mv4
-            ln_t[h]["rs"] = rs
+        def moments(pool, source, tiles):
+            stats = pool.tile([P, tiles, 6], F32, name="stats", tag="stats")
+            mean_var = pool.tile([P, tiles, 2], F32, name="mean_var", tag="mean_var")
+            for j in range(tiles):
+                nc.vector.bn_stats(out=stats[:, j, :], in_=source[:, j, :])
+            for j in range(tiles):
+                nc.vector.bn_aggr(out=mean_var[:, j, :], in_=stats[:, j, :])
+            return mean_var
 
-        def gain(h):
-            t1 = fin.tile([P, NJ, HD], F32, name="t1h", tag="t1h")
-            for j in range(NJ):
+        def token_moments(h):
+            mean_var = moments(small, head[h]["on_tokens"], TILES)
+            head[h]["mean_var"] = mean_var
+            head[h]["variance"] = mean_var[:, :, 1]
+
+        def rstd(h):
+            shifted = small.tile([P, TILES], F32, name="shifted", tag="shifted")
+            engine = nc.gpsimd if h < LAST - 1 else nc.vector
+            engine.tensor_scalar(
+                out=shifted[:], in0=head[h]["variance"], scalar1=EPS, scalar2=None, op0=ALU.add
+            )
+            root = small.tile([P, TILES], F32, name="root", tag="root")
+            nc.gpsimd.tensor_tensor(out=root[:], in0=shifted[:], in1=minus_half[:], op=ALU.pow)
+            head[h]["rstd"] = root
+
+        def centre_and_gain(dst, source, mean_var, h, tiles):
+            for j in range(tiles):
                 nc.vector.scalar_tensor_tensor(
-                    out=t1[:, j, :], in0=ln_t[h]["pb"][:, j, :], scalar=ln_t[h]["mv"][:, j, 0:1],
-                    in1=dw_bc[:, HD * h : HD * (h + 1)], op0=ALU.subtract, op1=ALU.mult,
+                    out=dst[:, j, :], in0=source[:, j, :], scalar=mean_var[:, j, 0:1],
+                    in1=gain_rows[:, HD * h : HD * (h + 1)], op0=ALU.subtract, op1=ALU.mult,
                 )
-            ln_t[h]["cw"] = t1
+
+        def token_gain(h):
+            result = fin.tile([P, TILES, HD], F32, name="gained", tag="gained")
+            centre_and_gain(result, head[h]["on_tokens"], head[h]["mean_var"], h, TILES)
+            head[h]["gained"] = result
+
+        def scale_add_store(dst, source, root, h, j0, tiles):
+            for j in range(tiles):
+                nc.vector.scalar_tensor_tensor(
+                    out=dst[:, j, :], in0=source[:, j, :], scalar=root[:, j : j + 1],
+                    in1=bias_rows[:, HD * h : HD * (h + 1)], op0=ALU.mult, op1=ALU.add,
+                )
+            view = out[0, h].rearrange("(p j) d -> p j d", j=TILES)
+            nc.sync.dma_start(out=view[:, j0 : j0 + tiles, :], in_=dst[:])
 
         def finish(h):
-            s = ln_t[h]
-            o = fin.tile([P, NJ, HD], F32, name="o", tag="o")
-            for j in range(NJ):
-                nc.vector.scalar_tensor_tensor(
-                    out=o[:, j, :], in0=s["cw"][:, j, :], scalar=s["rs"][:, j : j + 1],
-                    in1=db_bc[:, HD * h : HD * (h + 1)], op0=ALU.mult, op1=ALU.add,
-                )
-            nc.sync.dma_start(out=out[0, h].rearrange("(p j) d -> p j d", j=NJ), in_=o[:])
+            result = fin.tile([P, TILES, HD], F32, name="result", tag="result")
+            scale_add_store(result, head[h]["gained"], head[h]["rstd"], h, 0, TILES)
+        half = {}
 
-        last = {}
-        hd3 = slice(HD * (H - 1), HD * H)
+        def first_half_product():
+            bank = ps_turn.tile([P, HALF], F32, name="half_product", tag="turn")
+            second_passes(bank, LAST, slice(0, HALF))
+            on_channels = tail.tile([P, HALF], F32, name="half_on_channels", tag="half_on_channels")
+            add_proj_bias(on_channels, bank, LAST)
+            half["on_channels"] = on_channels
 
-        def last_matmuls(j0, j1):
-            pc, pscale = w_ops[unit_of_head[H - 1]]
-            n = j1 - j0
-            p_ps = ps_tr.tile([P, n, HD], F32, name="p_ps", tag="tr")
-            for j in range(j0, j1):
-                for c in range(NC):
-                    gc, gs = g_ops[NC * (H - 1) + c]
-                    nc.tensor.matmul_mx(
-                        out=p_ps[:, j - j0, :],
-                        lhsT=gc[:, P * j : P * (j + 1)].bitcast(FP8X4), lhsT_scale=gs[:, P * j : P * (j + 1)],
-                        rhs=pc[:, P * c : P * (c + 1)].bitcast(FP8X4), rhs_scale=pscale[:, P * c : P * (c + 1)],
-                        start=(c == 0), stop=(c == NC - 1),
-                    )
-            last[j0] = {"n": n, "p": p_ps}
+        def first_half_squares():
+            bank = ps_second.tile([P, HALF], F32, name="half_centred", tag="second")
+            nc.tensor.matmul(bank[:], centring[:], half["on_channels"][:], start=True, stop=True)
+            squares = tail.tile([P, HALF], F32, name="half_squares", tag="half_squares")
+            nc.scalar.activation(out=squares[:], in_=bank[:], func=ACT.Square)
+            half["squares"] = squares
 
-        def last_biased(j0):
-            n = last[j0]["n"]
-            pb = tail.tile([P, n, HD], F32, name="pb", tag="pb")
-            nc.vector.tensor_tensor(
-                out=pb[:], in0=last[j0]["p"][:], in1=pb_bc[:].unsqueeze(1).to_broadcast([P, n, HD]), op=ALU.add
-            )
-            last[j0]["pb"] = pb
-
-        def last_stats(j0):
-            n = last[j0]["n"]
-            st4 = tail.tile([P, n, 6], F32, name="st4", tag="st4")
-            mv4 = tail.tile([P, n, 2], F32, name="mv4", tag="mv4")
-            for j in range(n):
-                nc.vector.bn_stats(out=st4[:, j, :], in_=last[j0]["pb"][:, j, :])
-            for j in range(n):
-                nc.vector.bn_aggr(out=mv4[:, j, :], in_=st4[:, j, :])
-            rs4 = tail.tile([P, n, 1], F32, name="rs4", tag="rs4")
+        def last_rstd(variance_of_tiles):
+            root = tail.tile([P, 2], F32, name="last_root", tag="last_root")
             nc.scalar.activation(
-                out=rs4[:], in_=mv4[:, :, 1:2], func=ACT.Abs_reciprocal_sqrt, bias=eps_col[:], scale=1.0
+                out=root[:], in_=variance_of_tiles, func=ACT.Abs_reciprocal_sqrt, bias=eps[:], scale=1.0
             )
-            last[j0]["mv"] = mv4
-            last[j0]["rs"] = rs4
-
-        def last_gain(j0):
-            n = last[j0]["n"]
-            t1 = tail.tile([P, n, HD], F32, name="t1", tag="t1")
-            for j in range(n):
-                nc.vector.scalar_tensor_tensor(
-                    out=t1[:, j, :], in0=last[j0]["pb"][:, j, :], scalar=last[j0]["mv"][:, j, 0:1], in1=dw_bc[:, hd3],
-                    op0=ALU.subtract, op1=ALU.mult,
-                )
-            last[j0]["t1"] = t1
-
-        def last_finish(j0):
-            n = last[j0]["n"]
-            o = tail.tile([P, n, HD], F32, name="o3", tag="o3")
-            for j in range(n):
-                nc.vector.scalar_tensor_tensor(
-                    out=o[:, j, :], in0=last[j0]["t1"][:, j, :], scalar=last[j0]["rs"][:, j, :], in1=db_bc[:, hd3],
-                    op0=ALU.mult, op1=ALU.add,
-                )
-            nc.sync.dma_start(out=out[0, H - 1].rearrange("(p j) d -> p j d", j=NJ)[:, j0 : j0 + n, :], in_=o[:])
-
-        half = T // 2
-
-        def first_half():
-            h = H - 1
-            pc, pscale = w_ops[unit_of_head[h]]
-            pt_ps = ps_tr.tile([P, half], F32, name="pt_half_ps", tag="tr")
-            for c in range(NC):
-                gc, gs = g_ops[NC * h + c]
-                nc.tensor.matmul_mx(
-                    out=pt_ps[:],
-                    lhsT=pc[:, P * c : P * (c + 1)].bitcast(FP8X4), lhsT_scale=pscale[:, P * c : P * (c + 1)],
-                    rhs=gc[:, 0:half].bitcast(FP8X4), rhs_scale=gs[:, 0:half],
-                    start=(c == 0), stop=(c == NC - 1),
-                )
-            pt = tail.tile([P, half], F32, name="pt_half", tag="pt_half")
-            nc.scalar.activation(
-                out=pt[:], in_=pt_ps[:], func=ACT.Identity, bias=cols[:, 4, 24 + h : 25 + h], scale=1.0
-            )
-            last["pt"] = pt
-
-        def first_half_centre():
-            pt = last["pt"]
-            ct_ps = ps_pj.tile([P, half], F32, name="ct_half_ps", tag="pj")
-            nc.tensor.matmul(ct_ps[:], cmat[:], pt[:], start=True, stop=True)
-            sq = tail.tile([P, half], F32, name="sq_half", tag="sq_half")
-            nc.scalar.activation(out=sq[:], in_=ct_ps[:], func=ACT.Square)
-            last["sq"] = sq
+            return root
 
         def first_half_gain():
-            cw_ps = ps_tr.tile([P, 2, HD], F32, name="cw_half_ps", tag="tr")
-            vs_ps = ps_pj.tile([P, 2], F32, name="vs_half_ps", tag="pj")
+            bank = ps_turn.tile([P, 2, HD], F32, name="half_gained", tag="turn")
+            averages = ps_second.tile([P, 2], F32, name="half_variance", tag="second")
+            gained(bank, half["on_channels"], LAST, 2)
+            average_squares(averages, half["squares"], 2)
+            half["gained"] = bank
+            half["variance"] = averages[:]
+
+        def second_half_product():
+            bank = ps_turn.tile([P, 2, HD], F32, name="second_half", tag="turn")
+            codes_w, scales_w = weight_ops[unit_of_head[LAST]]
             for j in range(2):
-                nc.tensor.matmul(
-                    cw_ps[:, j, :], last["pt"][:, P * j : P * (j + 1)], cdw[:, H - 1, :], start=True, stop=True
-                )
-            for j in range(2):
-                nc.tensor.matmul(
-                    vs_ps[:, j : j + 1], last["sq"][:, P * j : P * (j + 1)], inv_col[:], start=True, stop=True
-                )
-            rs = tail.tile([P, 2], F32, name="rs_half", tag="rs_half")
-            nc.scalar.activation(
-                out=rs[:], in_=vs_ps[:], func=ACT.Abs_reciprocal_sqrt, bias=eps_col[:], scale=1.0
+                tokens = slice(HALF + P * j, HALF + P * (j + 1))
+                for c in range(GROUPS):
+                    codes, scales = gelu_ops[GROUPS * LAST + c]
+                    cols = slice(P * c, P * (c + 1))
+                    nc.tensor.matmul_mx(
+                        out=bank[:, j, :], lhsT=codes[:, tokens].bitcast(FP8X4), lhsT_scale=scales[:, tokens],
+                        rhs=codes_w[:, cols].bitcast(FP8X4), rhs_scale=scales_w[:, cols],
+                        start=(c == 0), stop=(c == GROUPS - 1),
+                    )
+            half["product"] = bank
+
+        def second_half_norm():
+            biased_rows = tail.tile([P, 2, HD], F32, name="biased_rows", tag="biased_rows")
+            nc.vector.tensor_tensor(
+                out=biased_rows[:], in0=half["product"][:],
+                in1=last_proj_bias[:].unsqueeze(1).to_broadcast([P, 2, HD]), op=ALU.add,
             )
-            last["cw"] = cw_ps
-            last["rs"] = rs
+            mean_var = moments(tail, biased_rows, 2)
+            root = last_rstd(mean_var[:, :, 1])
+            result = tail.tile([P, 2, HD], F32, name="last_gained", tag="last_gained")
+            centre_and_gain(result, biased_rows, mean_var, LAST, 2)
+            return result, root
 
-        def first_half_finish():
-            o = tail.tile([P, 2, HD], F32, name="o_half", tag="o3")
-            for j in range(2):
-                nc.vector.scalar_tensor_tensor(
-                    out=o[:, j, :], in0=last["cw"][:, j, :], scalar=last["rs"][:, j : j + 1], in1=db_bc[:, hd3],
-                    op0=ALU.mult, op1=ALU.add,
-                )
-            nc.sync.dma_start(out=out[0, H - 1].rearrange("(p j) d -> p j d", j=NJ)[:, 0:2, :], in_=o[:])
+        def finish_half(source, root, j0):
+            result = tail.tile([P, 2, HD], F32, name="last_result", tag="last_result")
+            scale_add_store(result, source, root, LAST, j0, 2)
 
-        norm = []
-        xsum = const.tile([P, NJ], F32, name="xsum")
-        xnm = const.tile([P, NJ], F32, name="xnm")
-        xss = const.tile([P, NJ], F32, name="xss")
-        xve = const.tile([P, NJ], F32, name="xve")
-        xrs = const.tile([P, NJ], F32, name="xrs")
+        sums = const.tile([P, TILES], F32, name="sums")
+        minus_means = const.tile([P, TILES], F32, name="minus_means")
+        square_sums = const.tile([P, TILES], F32, name="square_sums")
+        shifted_vars = const.tile([P, TILES], F32, name="shifted_vars")
+        rstds = const.tile([P, TILES], F32, name="rstds")
+        summed = []
+        x_banks = []
 
-        def x_add(j):
+        def add_streams(j):
             s = xpool.tile([P, D], F32, name="s", tag="s", bufs=4)
             nc.vector.scalar_tensor_tensor(
                 out=s[:], in0=xt_sb[:, j, :], scalar=1.0, in1=xe_sb[:, j, :], op0=ALU.mult, op1=ALU.add,
-                accum_out=xsum[:, j : j + 1],
+                accum_out=sums[:, j : j + 1],
             )
-            sq = xpool.tile([P, D], F32, name="xsq", tag="xsq", bufs=2)
+            squares = xpool.tile([P, D], F32, name="x_squares", tag="x_squares", bufs=2)
             nc.scalar.activation(
-                out=sq[:], in_=s[:], func=ACT.Square, bias=xsum[:, j : j + 1], scale=-1.0 * D,
-                accum_out=xss[:, j : j + 1],
+                out=squares[:], in_=s[:], func=ACT.Square, bias=sums[:, j : j + 1], scale=-1.0 * D,
+                accum_out=square_sums[:, j : j + 1],
             )
-            norm.append(s)
+            summed.append(s)
 
-        def x_rstd(js):
+        def first_rstd(js):
             nc.vector.tensor_scalar(
-                out=xve[:, js], in0=xss[:, js], scalar1=1.0 / D**3, scalar2=EPS, op0=ALU.mult, op1=ALU.add
+                out=shifted_vars[:, js], in0=square_sums[:, js], scalar1=1.0 / D**3, scalar2=EPS,
+                op0=ALU.mult, op1=ALU.add,
             )
-            nc.vector.tensor_scalar(
-                out=xnm[:, js], in0=xsum[:, js], scalar1=-1.0 / D, scalar2=None, op0=ALU.mult
+            nc.gpsimd.tensor_scalar(
+                out=minus_means[:, js], in0=sums[:, js], scalar1=-1.0 / D, scalar2=None, op0=ALU.mult
             )
-            nc.gpsimd.tensor_tensor(out=xrs[:, js], in0=xve[:, js], in1=neg_half4[:, js], op=ALU.pow)
+            nc.gpsimd.tensor_tensor(out=rstds[:, js], in0=shifted_vars[:, js], in1=minus_half[:, js], op=ALU.pow)
 
-        xps_t = []
-
-        def x_norm(j):
-            s = norm[j]
-            xh = xpool.tile([P, D], F32, name="xh", tag="xh", bufs=4)
+        def normalise(j):
+            normed = xpool.tile([P, D], F32, name="normed", tag="normed", bufs=4)
             nc.vector.tensor_scalar(
-                out=xh[:].rearrange("p (u e q) -> p u e q", u=2, e=2),
-                in0=s[:].rearrange("p (u q e) -> p u e q", u=2, e=2),
-                scalar1=xnm[:, j : j + 1], scalar2=xrs[:, j : j + 1], op0=ALU.add, op1=ALU.mult,
+                out=normed[:].rearrange("p (u e q) -> p u e q", u=2, e=2),
+                in0=summed[j][:].rearrange("p (u q e) -> p u e q", u=2, e=2),
+                scalar1=minus_means[:, j : j + 1], scalar2=rstds[:, j : j + 1], op0=ALU.add, op1=ALU.mult,
             )
-            for t in range(4):
+            for t in range(PACK):
                 if j == 0:
-                    xps = ps_fc.tile([P, T], F32, name="xps", tag="fc")
-                    xps_t.append(xps)
-                nc.tensor.transpose(xps_t[t][:, P * j : P * (j + 1)], xh[:, P * t : P * (t + 1)], ident_f[:])
+                    bank = ps_first.tile([P, T], F32, name="x_bank", tag="first")
+                    x_banks.append(bank)
+                tokens = slice(P * j, P * (j + 1))
+                nc.tensor.transpose(x_banks[t][:, tokens], normed[:, P * t : P * (t + 1)], ident_f[:])
 
-        def x_affine(t, on_vector):
+        def gain_and_bias(t, on_vector):
+            gain, bias = columns[:, t, 0:1], columns[:, t, 1:2]
             if on_vector:
                 nc.vector.tensor_scalar(
-                    out=x2p[:, t, :], in0=xps_t[t][:], scalar1=cols[:, t, 0:1], scalar2=cols[:, t, 1:2],
-                    op0=ALU.mult, op1=ALU.add,
+                    out=x2_planar[:, t, :], in0=x_banks[t][:], scalar1=gain, scalar2=bias, op0=ALU.mult, op1=ALU.add
                 )
             else:
                 nc.scalar.activation(
-                    out=x2p[:, t, :], in_=xps_t[t][:], func=ACT.Identity, bias=cols[:, t, 1:2], scale=cols[:, t, 0:1]
+                    out=x2_planar[:, t, :], in_=x_banks[t][:], func=ACT.Identity, bias=bias, scale=gain
                 )
-
-        def copies(n, on_vector):
-            for i in range(n):
-                if k["copies"] < 40:
-                    copy_block(on_vector)
-                    transposes_ahead(NTR)
 
         ctx.enter_context(tc.manual_schedule())
-        warm_ps = ps_fc.tile([P, T], F32, name="warm_ps", tag="fc")
-        for j in range(NJ):
-            nc.tensor.matmul(warm_ps[:], ident_bf[:], xt_sb[:, j, :], start=True, stop=True)
-            nc.tensor.matmul(warm_ps[:], ident_bf[:], xe_sb[:, j, :], start=True, stop=True)
-        transposes_ahead(2)
-        x_add(0)
-        x_add(1)
-        x_add(2)
-        x_rstd(slice(0, 2))
-        x_add(3)
-        for t in range(4):
+
+        unread = ps_first.tile([P, T], F32, name="unread", tag="first")
+        for j in range(TILES):
+            nc.tensor.matmul(unread[:], ident_bf[:], xt_sb[:, j, :], start=True, stop=True)
+            nc.tensor.matmul(unread[:], ident_bf[:], xe_sb[:, j, :], start=True, stop=True)
+
+        turn_blocks(2)
+        add_streams(0)
+        add_streams(1)
+        add_streams(2)
+        first_rstd(slice(0, 2))
+        add_streams(3)
+        for t in range(PACK):
             u, e = divmod(t, 2)
-            nc.tensor.transpose(cols_ps[:, t, :], vec_a[:, 256 * u + e : 256 * (u + 1) : 2], ident_bf[:])
-        nc.tensor.transpose(cols_ps[:, 4, :], vec_a[:, 0:P], ident_bf[:])
-        transposes_ahead(3)
-        x_norm(0)
-        x_norm(1)
-        x_rstd(slice(2, 4))
-        nc.vector.tensor_copy(out=cols[:], in_=cols_ps[:, :, 0:28])
-        copies(1, False)
-        copies(1, True)
-        x_norm(2)
-        x_norm(3)
-        copies(2, False)
-        quantise_ready_unit()
-        for t in range(4):
-            x_affine(t, t % 2 == 1)
-        nc.vector.tensor_copy(
-            out=x2g[:].rearrange("p (n i) t -> p n t i", i=4),
-            in_=x2p[:].rearrange("p t (n i) -> p n t i", i=4),
-        )
-        nc.vector.quantize_mx(out=xc[:].bitcast(FP8X4), scales=xs[:], in_=x2g[:].rearrange("p n t -> p (n t)"))
-        copies(3, False)
-        copy_block(False)
-        quantise_ready_unit()
-        first_matmuls_ahead(0)
-        quantise_ready_unit()
-        transposes_ahead(NTR)
+            nc.tensor.transpose(columns_ps[:, t, :], vectors[:, 256 * u + e : 256 * (u + 1) : 2], ident_bf[:])
+        nc.tensor.transpose(columns_ps[:, 4, :], vectors[:, 0:P], ident_bf[:])
+        turn_blocks(TURN_BANKS)
+        normalise(0)
+        normalise(1)
+        first_rstd(slice(2, 4))
+        nc.vector.tensor_copy(out=columns[:], in_=columns_ps[:, :, 0:28])
+        copy_and_turn(on_vector=False)
+        copy_and_turn(on_vector=True)
+        normalise(2)
+        normalise(3)
+        for i in range(2):
+            copy_and_turn(on_vector=False)
+        quantise_unit_if_copied()
+        for t in range(PACK):
+            gain_and_bias(t, on_vector=(t % 2 == 1))
+        halves = (slice(0, HALF), slice(HALF, T))
+        for tokens in halves:
+            regroup(x2_words[:, tokens, :], x2_planar[:, :, tokens])
+        for tokens in halves:
+            nc.vector.quantize_mx(
+                out=x2_codes[:, tokens].bitcast(FP8X4), scales=x2_scales[:, tokens],
+                in_=x2_words[:, tokens, :].rearrange("p n t -> p (n t)"),
+            )
+
+        for i in range(3):
+            copy_and_turn(on_vector=False)
+        copy_block(on_vector=False)
+        quantise_unit_if_copied()
+        first_passes(0)
+        quantise_unit_if_copied()
+        turn_blocks(TURN_BANKS)
         nc.gpsimd.tensor_scalar(
-            out=cmat[:], in0=ident_f[:],
-            scalar1=1.0, scalar2=-1.0 / HD, op0=ALU.mult, op1=ALU.add,
+            out=centring[:], in0=ident_f[:], scalar1=1.0, scalar2=-1.0 / HD, op0=ALU.mult, op1=ALU.add
         )
         nc.gpsimd.tensor_tensor(
-            out=cdw[:], in0=cmat[:].unsqueeze(1).to_broadcast([P, H, HD]),
-            in1=dw_bc[:].rearrange("p (h d) -> p h d", h=H), op=ALU.mult
+            out=centring_gain[:], in0=centring[:].unsqueeze(1).to_broadcast([P, H, HD]),
+            in1=gain_rows[:].rearrange("p (h d) -> p h d", h=H), op=ALU.mult,
         )
 
-        for h in range(H - 1):
-            r = NC * h + 5
-            hooks[(r, 1)] = partial(second_matmul, h)
-            hooks[(r + 1, 0)] = partial(biased, h)
-            if h < H - 2:
-                turn_back_at[r + 2] = h
-            else:
-                hooks[(r + 1, 1)] = partial(centre, h)
-                hooks[(r + 2, 0)] = partial(squared, h)
-                hooks[(r + 2, 1)] = partial(variance, h)
-                hooks[(r + 1, 2)] = partial(centred_gain, h)
+        for h in range(LAST):
+            r = GROUPS * h + 5
+            at(r, 1, partial(second_product, h))
+            at(r + 1, 0, partial(biased, h))
+        for r in range(ALL_GROUPS - 1):
+            at(r, 0, partial(turn_blocks, TURN_BANKS))
+        for h in range(LAST - 1):
+            at(GROUPS * h + 7, 0, partial(turned_back, h))
+        at(14, 0, partial(centred, LAST - 1))
+        at(14, 3, partial(squared, LAST - 1))
+        at(14, 3, partial(centred_gain, LAST - 1))
+        at(15, 0, partial(variance, LAST - 1))
 
-        for r in range(15):
-            h, step = divmod(r - 5, NC)
-            for i in range(S_COPIES[r]):
-                copy_block(False)
-            gelus(r, 0, NJ)
-            if r:
-                regroup(r - 1, 0, NJ)
-                ready = k["copies"] // 2
-                for i in range(V_COPIES[r]):
-                    copy_block(True)
-                if r >= 8 and r % NC == 0:
-                    finish(r // NC - 2)
-                if h >= 0 and step == 2:
-                    stats(h)
-                if len(w_ops) < ready:
-                    quantise_ready_unit()
-                quantise_g(r - 1, 0, NJ)
-                if h >= 0 and step == 2:
-                    gain(h)
-                quantise_ready_unit()
-            else:
-                for i in range(V_COPIES[r]):
-                    copy_block(True)
-                quantise_ready_unit()
-        warm_tail = ps_tr.tile([P, 2 * P], F32, name="warm_tail", tag="tr")
+        for r in range(ALL_GROUPS - 1):
+            blocks = min(3 - r % 2, BLOCKS - count["copied"])
+            on_vector = min(2 if r == 0 else 1 if r < 7 else int(r in (8, 10, 12)), blocks)
+            norm_of = {7: 0, 11: 1}.get(r)
+            for i in range(blocks - on_vector):
+                copy_block(on_vector=False)
+            gelus(r, 0, TILES)
+            if r == 14:
+                regroup_gelus(r - 1, 0, 2)
+                regroup_gelus(r - 1, 2, TILES)
+            elif r > 0:
+                regroup_gelus(r - 1, 0, TILES)
+            whole = count["copied"] // 2
+            for i in range(on_vector):
+                copy_block(on_vector=True)
+            if r in (8, 12):
+                finish(r // GROUPS - 2)
+            if norm_of is not None:
+                token_moments(norm_of)
+                rstd(norm_of)
+            if len(weight_ops) < whole or r == 0:
+                quantise_unit_if_copied()
+            if r == 14:
+                quantise_gelus(r - 1, 0, 2)
+                quantise_gelus(r - 1, 2, TILES)
+            elif r > 0:
+                quantise_gelus(r - 1, 0, TILES)
+                if norm_of is not None:
+                    token_gain(norm_of)
+                quantise_unit_if_copied()
 
-        def keep_warm(j0, j1):
-            for t in range(4):
-                nc.tensor.matmul(
-                    warm_tail[:], ident_bf[:], gp_t[15][:, t, P * j0 : P * j1], start=True, stop=True
-                )
-
-        gelus(15, 0, 2)
-        keep_warm(0, 2)
-        regroup(14, 0, NJ)
-        quantise_g(14, 0, NJ)
-        gelus(15, 2, 4)
-        keep_warm(2, 4)
-        table_out = const.tile([P, 1], F32, name="table_out")
+        last_group = ALL_GROUPS - 1
+        unread_tail = ps_turn.tile([P, HALF], F32, name="unread_tail", tag="turn")
+        gelus(last_group, 0, 2)
+        regroup_gelus(last_group - 1, 0, 2)
+        regroup_gelus(last_group - 1, 2, TILES)
+        quantise_gelus(last_group - 1, 0, 2)
+        quantise_gelus(last_group - 1, 2, TILES)
+        gelus(last_group, 2, 4)
+        for t in range(PACK):
+            nc.tensor.matmul(
+                unread_tail[:], ident_bf[:], gelu_planar[last_group][:, t, HALF:T], start=True, stop=True
+            )
+        table_loader = const.tile([P, 1], F32, name="table_loader")
         nc.scalar.activation(
-            out=table_out[:], in_=gp_t[15][:, 3, T - 1 : T], func=ACT.Abs_reciprocal_sqrt, bias=1.0, scale=0.0
+            out=table_loader[:], in_=gelu_planar[last_group][:, PACK - 1, T - 1 : T], func=ACT.Abs_reciprocal_sqrt,
+            bias=1.0, scale=0.0,
         )
-        regroup(15, 0, 2)
-        rstd(2)
-        quantise_g(15, 0, 2)
-        regroup(15, 2, 4)
-        first_half()
-        quantise_g(15, 2, 4)
-        last_matmuls(2, 4)
-        first_half_centre()
+        regroup_gelus(last_group, 0, 2)
+        rstd(LAST - 1)
+        quantise_gelus(last_group, 0, 2)
+        regroup_gelus(last_group, 2, 3)
+        regroup_gelus(last_group, 3, 4)
+        first_half_product()
+        quantise_gelus(last_group, 2, 3)
+        quantise_gelus(last_group, 3, 4)
+        second_half_product()
+        first_half_squares()
         first_half_gain()
-        finish(2)
-        last_biased(2)
-        last_stats(2)
-        last_gain(2)
-        first_half_finish()
-        last_finish(2)
-        assert k["copies"] == 40 and len(w_ops) == 20 and k["fc"] == 64
+        finish(LAST - 1)
+        gained_rows, root = second_half_norm()
+        first_root = last_rstd(half["variance"])
+        finish_half(gained_rows, root, 2)
+        finish_half(half["gained"], first_root, 0)

from contextlib import ExitStack
from functools import partial

import concourse.mybir as mybir
from concourse.masks import make_identity

F32 = mybir.dt.float32
BF16 = mybir.dt.bfloat16
U32 = mybir.dt.uint32
U8 = mybir.dt.uint8
FP8X4 = mybir.dt.float8_e4m3fn_x4
ACT = mybir.ActivationFunctionType
ALU = mybir.AluOpType

P = 128
T = 512
D = 512
H = 4
FF = 2048
HD = 128
EPS = 1e-5
FLOPS = 2 * T * D * FF * H + 2 * T * FF * HD * H

TILES = T // P
GROUPS = FF // 512
ALL_GROUPS = H * GROUPS
PACK = 4
RUN = 4
HALF = T // 2
LAST = H - 1

TURN_BANKS = 3
FIRST_BANKS = 4

PROJ_AT = {6: 0, 11: 1, 16: 2, 19: 3}
UNITS = 20
BLOCKS = 2 * UNITS
NORM_VECTORS_AFTER = 13


def tile_tftdictblock_pa_kernel(
    tc, xt_new, xe, ln2_w, ln2_b, fc_w, fc_b, proj_w, proj_b, dln_w, dln_b, out
):
    nc = tc.nc
    with ExitStack() as ctx:
        const = ctx.enter_context(tc.tile_pool(name="const", bufs=1))
        xpool = ctx.enter_context(tc.tile_pool(name="xpool", bufs=1))
        small = ctx.enter_context(tc.tile_pool(name="small", bufs=4))
        rawp = ctx.enter_context(tc.tile_pool(name="rawp", bufs=12))
        wgp = ctx.enter_context(tc.tile_pool(name="wgp", bufs=8))
        wcp = ctx.enter_context(tc.tile_pool(name="wcp", bufs=12))
        pcp = ctx.enter_context(tc.tile_pool(name="pcp", bufs=4))
        gpp = ctx.enter_context(tc.tile_pool(name="gpp", bufs=3))
        ggp = ctx.enter_context(tc.tile_pool(name="ggp", bufs=2))
        gcp = ctx.enter_context(tc.tile_pool(name="gcp", bufs=8))
        fin = ctx.enter_context(tc.tile_pool(name="fin", bufs=2))
        tail = ctx.enter_context(tc.tile_pool(name="tail", bufs=3))
        ps_turn = ctx.enter_context(tc.psum_pool(name="ps_turn", bufs=TURN_BANKS))
        ps_first = ctx.enter_context(tc.psum_pool(name="ps_first", bufs=FIRST_BANKS))
        ps_second = ctx.enter_context(tc.psum_pool(name="ps_second", bufs=1))

        unit_kind = []
        unit_of_group = []
        unit_of_head = {}
        for pos in range(UNITS):
            if pos in PROJ_AT:
                unit_of_head[PROJ_AT[pos]] = pos
                unit_kind.append(("proj", PROJ_AT[pos]))
            else:
                unit_kind.append(("fc", len(unit_of_group)))
                unit_of_group.append(pos)

        vectors = const.tile([P, 512], BF16, name="vectors")
        nc.gpsimd.memset(vectors[:], 0.0)
        nc.scalar.dma_start(out=vectors[0:1, :], in_=ln2_w.rearrange("(o d) -> o d", o=1))
        nc.scalar.dma_start(out=vectors[1:2, :], in_=ln2_b.rearrange("(o d) -> o d", o=1))
        nc.scalar.dma_start(out=vectors[8:24, :], in_=fc_b.rearrange("h (c x) -> (h c) x", x=512))
        nc.scalar.dma_start(out=vectors[24:28, 0:P], in_=proj_b)
        zero = const.tile([P, 1], F32, name="zero")
        gelu_of_zero = const.tile([P, 1], F32, name="gelu_of_zero")
        nc.vector.memset(zero[:], 0.0)
        nc.scalar.activation(out=gelu_of_zero[:], in_=zero[:], func=ACT.Gelu)
        minus_half = const.tile([P, TILES], F32, name="minus_half")
        mean_weight = const.tile([P, 1], F32, name="mean_weight")
        nc.vector.memset(mean_weight[:], 1.0 / HD)
        nc.vector.memset(minus_half[:], -0.5)
        eps = const.tile([P, 1], F32, name="eps")
        nc.vector.tensor_scalar(out=eps[:], in0=zero[:], scalar1=EPS, scalar2=None, op0=ALU.add)
        ident_bf = const.tile([P, P], BF16, name="ident_bf")
        ident_f = const.tile([P, P], F32, name="ident_f")
        make_identity(nc, ident_bf[:])
        make_identity(nc, ident_f[:])

        xt_view = xt_new.rearrange("b (p j) d -> p (b j) d", j=TILES)
        xe_view = xe.rearrange("b (p j) d -> p (b j) d", j=TILES)
        xt_sb = xpool.tile([P, TILES, D], BF16, name="xt_sb")
        xe_sb = xpool.tile([P, TILES, D], BF16, name="xe_sb")
        for js in (slice(0, 1), slice(1, 2), slice(2, 4)):
            nc.sync.dma_start(out=xt_sb[:, js, :], in_=xt_view[:, js, :])
            nc.sync.dma_start(out=xe_sb[:, js, :], in_=xe_view[:, js, :])

        raw_of_unit = []
        norm_vectors = []
        for pos in range(UNITS):
            kind, index = unit_kind[pos]
            raw = rawp.tile([P, 2048], BF16, name="raw", tag="raw")
            if kind == "fc":
                h, c = divmod(index, GROUPS)
                nc.sync.dma_start(
                    out=raw[:].rearrange("p (u x) -> p u x", u=2),
                    in_=fc_w[h, 512 * c : 512 * (c + 1), :].rearrange("(u p e) k -> p u (e k)", u=2, e=2),
                )
            else:
                nc.sync.dma_start(out=raw[:], in_=proj_w[index, :, :])
            raw_of_unit.append(raw)
            if pos == NORM_VECTORS_AFTER:
                for name, vec in (("gain_rows", dln_w), ("bias_rows", dln_b)):
                    rows = const.tile([P, H * HD], BF16, name=name)
                    nc.sync.dma_start(out=rows[:], in_=vec.rearrange("h d -> (h d)").partition_broadcast(P))
                    norm_vectors.append(rows)
        gain_rows, bias_rows = norm_vectors
        last_proj_bias = const.tile([P, HD], BF16, name="last_proj_bias")
        nc.sync.dma_start(out=last_proj_bias[:], in_=proj_b[LAST, :].partition_broadcast(P))

        columns_ps = ps_second.tile([P, 5, P], BF16, name="columns_ps", tag="second")
        columns = const.tile([P, 5, 28], F32, name="columns")

        x2_planar = xpool.tile([P, PACK, T], BF16, name="x2_planar")
        x2_words = xpool.tile([P, T, PACK], BF16, name="x2_words", align_bytes=64)
        x2_codes = xpool.tile([P, T], U32, name="x2_codes", align_bytes=64)
        x2_scales = xpool.tile([P, T], U8, name="x2_scales", align_bytes=64)

        turned = []
        weight_words = []
        weight_ops = []
        count = {"copied": 0, "first": 0}

        def turn_blocks(ahead):
            while len(turned) < min(count["copied"] + ahead, BLOCKS):
                unit, b = divmod(len(turned), 2)
                words = raw_of_unit[unit][:].bitcast(F32)
                bank = ps_turn.tile([P, 512], F32, name="bank", tag="turn")
                for q in range(4):
                    first = 512 * b + P * q
                    nc.tensor.transpose(bank[:, P * q : P * (q + 1)], words[:, first : first + P], ident_f[:])
                turned.append(bank)

        def copy_block(on_vector):
            unit, b = divmod(count["copied"], 2)
            if b == 0:
                words = wgp.tile([P, 2048], BF16, name="words", tag="words", align_bytes=64)
                weight_words.append(words)
            dst = weight_words[unit][:].bitcast(F32)[:, 512 * b : 512 * (b + 1)]
            dst = dst.rearrange("p (i f u) -> p i f u", i=2, u=2)
            src = turned[count["copied"]][:].rearrange("p (i u f) -> p i f u", i=2, u=2)
            if on_vector:
                nc.vector.tensor_copy(out=dst, in_=src)
            else:
                nc.scalar.copy(out=dst, in_=src)
            count["copied"] += 1

        def copy_and_turn(on_vector):
            copy_block(on_vector)
            turn_blocks(TURN_BANKS)

        def quantise_unit_if_copied():
            unit = len(weight_ops)
            if 2 * unit + 2 > count["copied"]:
                return
            pool = wcp if unit_kind[unit][0] == "fc" else pcp
            codes = pool.tile([P, 512], U32, name="codes", tag="codes", align_bytes=64)
            scales = pool.tile([P, 512], U8, name="scales", tag="scales", align_bytes=64)
            nc.vector.quantize_mx(out=codes[:].bitcast(FP8X4), scales=scales[:], in_=weight_words[unit][:])
            weight_ops.append((codes, scales))

        first_ps = {}
        gelu_planar = {}
        gelu_words = {}
        gelu_ops = {}

        def first_passes(emptied):
            while count["first"] < min(emptied + FIRST_BANKS, PACK * ALL_GROUPS):
                r, t = divmod(count["first"], PACK)
                if unit_of_group[r] >= len(weight_ops):
                    return
                codes, scales = weight_ops[unit_of_group[r]]
                product = ps_first.tile([P, T], F32, name="product", tag="first")
                cols = slice(P * t, P * (t + 1))
                nc.tensor.matmul_mx(
                    out=product[:], lhsT=codes[:, cols].bitcast(FP8X4), lhsT_scale=scales[:, cols],
                    rhs=x2_codes[:].bitcast(FP8X4), rhs_scale=x2_scales[:], start=True, stop=True,
                )
                first_ps[(r, t)] = product
                count["first"] += 1

        before_gelu = {}

        def at(r, t, step):
            before_gelu.setdefault((r, t), []).append(step)

        def gelus(r, j0, j1):
            if j0 == 0:
                planar = gpp.tile([P, PACK, T], BF16, name="planar", tag="planar")
                gelu_planar[r] = planar
            tokens = slice(P * j0, P * j1)
            for t in range(PACK):
                if j0 == 0:
                    for step in before_gelu.get((r, t), []):
                        step()
                first_passes(PACK * r + t)
                nc.scalar.activation(
                    out=gelu_planar[r][:, t, tokens], in_=first_ps[(r, t)][:, tokens], func=ACT.Gelu,
                    bias=columns[:, t, 8 + r : 9 + r], scale=1.0,
                )
                if j1 == TILES:
                    first_passes(PACK * r + t + 1)

        def regroup(dst, src):
            nc.vector.tensor_copy(
                out=dst.rearrange("p (n i) t -> p n t i", i=RUN), in_=src.rearrange("p t (n i) -> p n t i", i=RUN)
            )

        def regroup_gelus(r, j0, j1):
            if j0 == 0:
                words = ggp.tile([P, T, PACK], BF16, name="words_g", tag="words_g", align_bytes=64)
                gelu_words[r] = words
            tokens = slice(P * j0, P * j1)
            regroup(gelu_words[r][:, tokens, :], gelu_planar[r][:, :, tokens])

        def quantise_gelus(r, j0, j1):
            if j0 == 0:
                codes = gcp.tile([P, T], U32, name="codes_g", tag="codes_g", align_bytes=64)
                scales = gcp.tile([P, T], U8, name="scales_g", tag="scales_g", align_bytes=64)
                gelu_ops[r] = (codes, scales)
            codes, scales = gelu_ops[r]
            tokens = slice(P * j0, P * j1)
            nc.vector.quantize_mx(
                out=codes[:, tokens].bitcast(FP8X4), scales=scales[:, tokens],
                in_=gelu_words[r][:, tokens, :].rearrange("p n t -> p (n t)"),
            )

        head = {}
        centring = const.tile([P, HD], F32, name="centring")
        centring_gain = const.tile([P, H, HD], F32, name="centring_gain")

        def second_passes(bank, h, tokens):
            codes_w, scales_w = weight_ops[unit_of_head[h]]
            for c in range(GROUPS):
                codes, scales = gelu_ops[GROUPS * h + c]
                cols = slice(P * c, P * (c + 1))
                nc.tensor.matmul_mx(
                    out=bank[:], lhsT=codes_w[:, cols].bitcast(FP8X4), lhsT_scale=scales_w[:, cols],
                    rhs=codes[:, tokens].bitcast(FP8X4), rhs_scale=scales[:, tokens],
                    start=(c == 0), stop=(c == GROUPS - 1),
                )

        def add_proj_bias(out_tile, bank, h):
            nc.scalar.activation(
                out=out_tile[:], in_=bank[:], func=ACT.Identity, bias=columns[:, 4, 24 + h : 25 + h], scale=1.0
            )

        def second_product(h):
            bank = ps_second.tile([P, T], F32, name="product2", tag="second")
            second_passes(bank, h, slice(0, T))
            head[h] = {"product": bank}

        def biased(h):
            on_channels = fin.tile([P, T], F32, name="on_channels", tag="on_channels")
            add_proj_bias(on_channels, head[h]["product"], h)
            head[h]["on_channels"] = on_channels

        def centred(h):
            bank = ps_second.tile([P, T], F32, name="centred", tag="second")
            nc.tensor.matmul(bank[:], centring[:], head[h]["on_channels"][:], start=True, stop=True)
            head[h]["centred"] = bank

        def squared(h):
            squares = fin.tile([P, T], F32, name="squares", tag="squares")
            nc.scalar.activation(out=squares[:], in_=head[h]["centred"][:], func=ACT.Square)
            head[h]["squares"] = squares

        def average_squares(bank, squares, tiles):
            for j in range(tiles):
                nc.tensor.matmul(
                    bank[:, j : j + 1], squares[:, P * j : P * (j + 1)], mean_weight[:], start=True, stop=True
                )

        def gained(bank, on_channels, h, tiles):
            for j in range(tiles):
                nc.tensor.matmul(
                    bank[:, j, :], on_channels[:, P * j : P * (j + 1)], centring_gain[:, h, :], start=True, stop=True
                )

        def variance(h):
            bank = ps_second.tile([P, TILES], F32, name="variance", tag="second")
            average_squares(bank, head[h]["squares"], TILES)
            head[h]["variance"] = bank[:]

        def centred_gain(h):
            bank = ps_turn.tile([P, TILES, HD], F32, name="centred_gain", tag="turn")
            gained(bank, head[h]["on_channels"], h, TILES)
            head[h]["gained"] = bank

        def turned_back(h):
            bank = ps_second.tile([P, TILES, HD], F32, name="on_tokens", tag="second")
            for j in range(TILES):
                nc.tensor.transpose(bank[:, j, :], head[h]["on_channels"][:, P * j : P * (j + 1)], ident_f[:])
            head[h]["on_tokens"] = bank

        def moments(pool, source, tiles):
            stats = pool.tile([P, tiles, 6], F32, name="stats", tag="stats")
            mean_var = pool.tile([P, tiles, 2], F32, name="mean_var", tag="mean_var")
            for j in range(tiles):
                nc.vector.bn_stats(out=stats[:, j, :], in_=source[:, j, :])
            for j in range(tiles):
                nc.vector.bn_aggr(out=mean_var[:, j, :], in_=stats[:, j, :])
            return mean_var

        def token_moments(h):
            mean_var = moments(small, head[h]["on_tokens"], TILES)
            head[h]["mean_var"] = mean_var
            head[h]["variance"] = mean_var[:, :, 1]

        def rstd(h):
            shifted = small.tile([P, TILES], F32, name="shifted", tag="shifted")
            engine = nc.gpsimd if h < LAST - 1 else nc.vector
            engine.tensor_scalar(
                out=shifted[:], in0=head[h]["variance"], scalar1=EPS, scalar2=None, op0=ALU.add
            )
            root = small.tile([P, TILES], F32, name="root", tag="root")
            nc.gpsimd.tensor_tensor(out=root[:], in0=shifted[:], in1=minus_half[:], op=ALU.pow)
            head[h]["rstd"] = root

        def centre_and_gain(dst, source, mean_var, h, tiles):
            for j in range(tiles):
                nc.vector.scalar_tensor_tensor(
                    out=dst[:, j, :], in0=source[:, j, :], scalar=mean_var[:, j, 0:1],
                    in1=gain_rows[:, HD * h : HD * (h + 1)], op0=ALU.subtract, op1=ALU.mult,
                )

        def token_gain(h):
            result = fin.tile([P, TILES, HD], F32, name="gained", tag="gained")
            centre_and_gain(result, head[h]["on_tokens"], head[h]["mean_var"], h, TILES)
            head[h]["gained"] = result

        def scale_add_store(dst, source, root, h, j0, tiles):
            for j in range(tiles):
                nc.vector.scalar_tensor_tensor(
                    out=dst[:, j, :], in0=source[:, j, :], scalar=root[:, j : j + 1],
                    in1=bias_rows[:, HD * h : HD * (h + 1)], op0=ALU.mult, op1=ALU.add,
                )
            view = out[0, h].rearrange("(p j) d -> p j d", j=TILES)
            nc.sync.dma_start(out=view[:, j0 : j0 + tiles, :], in_=dst[:])

        def finish(h):
            result = fin.tile([P, TILES, HD], F32, name="result", tag="result")
            scale_add_store(result, head[h]["gained"], head[h]["rstd"], h, 0, TILES)
        half = {}

        def first_half_product():
            bank = ps_turn.tile([P, HALF], F32, name="half_product", tag="turn")
            second_passes(bank, LAST, slice(0, HALF))
            on_channels = tail.tile([P, HALF], F32, name="half_on_channels", tag="half_on_channels")
            add_proj_bias(on_channels, bank, LAST)
            half["on_channels"] = on_channels

        def first_half_squares():
            bank = ps_second.tile([P, HALF], F32, name="half_centred", tag="second")
            nc.tensor.matmul(bank[:], centring[:], half["on_channels"][:], start=True, stop=True)
            squares = tail.tile([P, HALF], F32, name="half_squares", tag="half_squares")
            nc.scalar.activation(out=squares[:], in_=bank[:], func=ACT.Square)
            half["squares"] = squares

        def last_rstd(variance_of_tiles):
            root = tail.tile([P, 2], F32, name="last_root", tag="last_root")
            nc.scalar.activation(
                out=root[:], in_=variance_of_tiles, func=ACT.Abs_reciprocal_sqrt, bias=eps[:], scale=1.0
            )
            return root

        def first_half_gain():
            bank = ps_turn.tile([P, 2, HD], F32, name="half_gained", tag="turn")
            averages = ps_second.tile([P, 2], F32, name="half_variance", tag="second")
            gained(bank, half["on_channels"], LAST, 2)
            average_squares(averages, half["squares"], 2)
            half["gained"] = bank
            half["variance"] = averages[:]

        def second_half_product():
            bank = ps_turn.tile([P, 2, HD], F32, name="second_half", tag="turn")
            codes_w, scales_w = weight_ops[unit_of_head[LAST]]
            for j in range(2):
                tokens = slice(HALF + P * j, HALF + P * (j + 1))
                for c in range(GROUPS):
                    codes, scales = gelu_ops[GROUPS * LAST + c]
                    cols = slice(P * c, P * (c + 1))
                    nc.tensor.matmul_mx(
                        out=bank[:, j, :], lhsT=codes[:, tokens].bitcast(FP8X4), lhsT_scale=scales[:, tokens],
                        rhs=codes_w[:, cols].bitcast(FP8X4), rhs_scale=scales_w[:, cols],
                        start=(c == 0), stop=(c == GROUPS - 1),
                    )
            half["product"] = bank

        def second_half_norm():
            biased_rows = tail.tile([P, 2, HD], F32, name="biased_rows", tag="biased_rows")
            nc.vector.tensor_tensor(
                out=biased_rows[:], in0=half["product"][:],
                in1=last_proj_bias[:].unsqueeze(1).to_broadcast([P, 2, HD]), op=ALU.add,
            )
            mean_var = moments(tail, biased_rows, 2)
            root = last_rstd(mean_var[:, :, 1])
            result = tail.tile([P, 2, HD], F32, name="last_gained", tag="last_gained")
            centre_and_gain(result, biased_rows, mean_var, LAST, 2)
            return result, root

        def finish_half(source, root, j0):
            result = tail.tile([P, 2, HD], F32, name="last_result", tag="last_result")
            scale_add_store(result, source, root, LAST, j0, 2)

        sums = const.tile([P, TILES], F32, name="sums")
        minus_means = const.tile([P, TILES], F32, name="minus_means")
        square_sums = const.tile([P, TILES], F32, name="square_sums")
        shifted_vars = const.tile([P, TILES], F32, name="shifted_vars")
        rstds = const.tile([P, TILES], F32, name="rstds")
        summed = []
        x_banks = []

        def add_streams(j):
            s = xpool.tile([P, D], F32, name="s", tag="s", bufs=4)
            nc.vector.scalar_tensor_tensor(
                out=s[:], in0=xt_sb[:, j, :], scalar=1.0, in1=xe_sb[:, j, :], op0=ALU.mult, op1=ALU.add,
                accum_out=sums[:, j : j + 1],
            )
            squares = xpool.tile([P, D], F32, name="x_squares", tag="x_squares", bufs=2)
            nc.scalar.activation(
                out=squares[:], in_=s[:], func=ACT.Square, bias=sums[:, j : j + 1], scale=-1.0 * D,
                accum_out=square_sums[:, j : j + 1],
            )
            summed.append(s)

        def first_rstd(js):
            nc.vector.tensor_scalar(
                out=shifted_vars[:, js], in0=square_sums[:, js], scalar1=1.0 / D**3, scalar2=EPS,
                op0=ALU.mult, op1=ALU.add,
            )
            nc.gpsimd.tensor_scalar(
                out=minus_means[:, js], in0=sums[:, js], scalar1=-1.0 / D, scalar2=None, op0=ALU.mult
            )
            nc.gpsimd.tensor_tensor(out=rstds[:, js], in0=shifted_vars[:, js], in1=minus_half[:, js], op=ALU.pow)

        def normalise(j):
            normed = xpool.tile([P, D], F32, name="normed", tag="normed", bufs=4)
            nc.vector.tensor_scalar(
                out=normed[:].rearrange("p (u e q) -> p u e q", u=2, e=2),
                in0=summed[j][:].rearrange("p (u q e) -> p u e q", u=2, e=2),
                scalar1=minus_means[:, j : j + 1], scalar2=rstds[:, j : j + 1], op0=ALU.add, op1=ALU.mult,
            )
            for t in range(PACK):
                if j == 0:
                    bank = ps_first.tile([P, T], F32, name="x_bank", tag="first")
                    x_banks.append(bank)
                tokens = slice(P * j, P * (j + 1))
                nc.tensor.transpose(x_banks[t][:, tokens], normed[:, P * t : P * (t + 1)], ident_f[:])

        def gain_and_bias(t, on_vector):
            gain, bias = columns[:, t, 0:1], columns[:, t, 1:2]
            if on_vector:
                nc.vector.tensor_scalar(
                    out=x2_planar[:, t, :], in0=x_banks[t][:], scalar1=gain, scalar2=bias, op0=ALU.mult, op1=ALU.add
                )
            else:
                nc.scalar.activation(
                    out=x2_planar[:, t, :], in_=x_banks[t][:], func=ACT.Identity, bias=bias, scale=gain
                )

        ctx.enter_context(tc.manual_schedule())

        unread = ps_first.tile([P, T], F32, name="unread", tag="first")
        for j in range(TILES):
            nc.tensor.matmul(unread[:], ident_bf[:], xt_sb[:, j, :], start=True, stop=True)
            nc.tensor.matmul(unread[:], ident_bf[:], xe_sb[:, j, :], start=True, stop=True)

        turn_blocks(2)
        add_streams(0)
        add_streams(1)
        add_streams(2)
        first_rstd(slice(0, 2))
        add_streams(3)
        for t in range(PACK):
            u, e = divmod(t, 2)
            nc.tensor.transpose(columns_ps[:, t, :], vectors[:, 256 * u + e : 256 * (u + 1) : 2], ident_bf[:])
        nc.tensor.transpose(columns_ps[:, 4, :], vectors[:, 0:P], ident_bf[:])
        turn_blocks(TURN_BANKS)
        normalise(0)
        normalise(1)
        first_rstd(slice(2, 4))
        nc.vector.tensor_copy(out=columns[:], in_=columns_ps[:, :, 0:28])
        copy_and_turn(on_vector=False)
        copy_and_turn(on_vector=True)
        normalise(2)
        normalise(3)
        for i in range(2):
            copy_and_turn(on_vector=False)
        quantise_unit_if_copied()
        for t in range(PACK):
            gain_and_bias(t, on_vector=(t % 2 == 1))
        halves = (slice(0, HALF), slice(HALF, T))
        for tokens in halves:
            regroup(x2_words[:, tokens, :], x2_planar[:, :, tokens])
        for tokens in halves:
            nc.vector.quantize_mx(
                out=x2_codes[:, tokens].bitcast(FP8X4), scales=x2_scales[:, tokens],
                in_=x2_words[:, tokens, :].rearrange("p n t -> p (n t)"),
            )

        for i in range(3):
            copy_and_turn(on_vector=False)
        copy_block(on_vector=False)
        quantise_unit_if_copied()
        first_passes(0)
        quantise_unit_if_copied()
        turn_blocks(TURN_BANKS)
        nc.gpsimd.tensor_scalar(
            out=centring[:], in0=ident_f[:], scalar1=1.0, scalar2=-1.0 / HD, op0=ALU.mult, op1=ALU.add
        )
        nc.gpsimd.tensor_tensor(
            out=centring_gain[:], in0=centring[:].unsqueeze(1).to_broadcast([P, H, HD]),
            in1=gain_rows[:].rearrange("p (h d) -> p h d", h=H), op=ALU.mult,
        )

        for h in range(LAST):
            r = GROUPS * h + 5
            at(r, 1, partial(second_product, h))
            at(r + 1, 0, partial(biased, h))
        for r in range(ALL_GROUPS - 1):
            at(r, 0, partial(turn_blocks, TURN_BANKS))
        for h in range(LAST - 1):
            at(GROUPS * h + 7, 0, partial(turned_back, h))
        at(14, 0, partial(centred, LAST - 1))
        at(14, 3, partial(squared, LAST - 1))
        at(14, 3, partial(centred_gain, LAST - 1))
        at(15, 0, partial(variance, LAST - 1))

        for r in range(ALL_GROUPS - 1):
            blocks = min(3 - r % 2, BLOCKS - count["copied"])
            on_vector = min(2 if r == 0 else 1 if r < 7 else int(r in (8, 10, 12)), blocks)
            norm_of = {7: 0, 11: 1}.get(r)
            for i in range(blocks - on_vector):
                copy_block(on_vector=False)
            gelus(r, 0, TILES)
            if r == 14:
                regroup_gelus(r - 1, 0, 2)
                regroup_gelus(r - 1, 2, TILES)
            elif r > 0:
                regroup_gelus(r - 1, 0, TILES)
            whole = count["copied"] // 2
            for i in range(on_vector):
                copy_block(on_vector=True)
            if r in (8, 12):
                finish(r // GROUPS - 2)
            if norm_of is not None:
                token_moments(norm_of)
                rstd(norm_of)
            if len(weight_ops) < whole or r == 0:
                quantise_unit_if_copied()
            if r == 14:
                quantise_gelus(r - 1, 0, 2)
                quantise_gelus(r - 1, 2, TILES)
            elif r > 0:
                quantise_gelus(r - 1, 0, TILES)
                if norm_of is not None:
                    token_gain(norm_of)
                quantise_unit_if_copied()

        last_group = ALL_GROUPS - 1
        unread_tail = ps_turn.tile([P, HALF], F32, name="unread_tail", tag="turn")
        gelus(last_group, 0, 2)
        regroup_gelus(last_group - 1, 0, 2)
        regroup_gelus(last_group - 1, 2, TILES)
        quantise_gelus(last_group - 1, 0, 2)
        quantise_gelus(last_group - 1, 2, TILES)
        gelus(last_group, 2, 4)
        for t in range(PACK):
            nc.tensor.matmul(
                unread_tail[:], ident_bf[:], gelu_planar[last_group][:, t, HALF:T], start=True, stop=True
            )
        table_loader = const.tile([P, 1], F32, name="table_loader")
        nc.scalar.activation(
            out=table_loader[:], in_=gelu_planar[last_group][:, PACK - 1, T - 1 : T], func=ACT.Abs_reciprocal_sqrt,
            bias=1.0, scale=0.0,
        )
        regroup_gelus(last_group, 0, 2)
        rstd(LAST - 1)
        quantise_gelus(last_group, 0, 2)
        regroup_gelus(last_group, 2, 3)
        regroup_gelus(last_group, 3, 4)
        first_half_product()
        quantise_gelus(last_group, 2, 3)
        quantise_gelus(last_group, 3, 4)
        second_half_product()
        first_half_squares()
        first_half_gain()
        finish(LAST - 1)
        gained_rows, root = second_half_norm()
        first_root = last_rstd(half["variance"])
        finish_half(gained_rows, root, 2)
        finish_half(half["gained"], first_root, 0)
